import numpy as np
import ml_dtypes


def mxq(x, axis, fmt="e4m3"):
    dtype, down = {"e4m3": (ml_dtypes.float8_e4m3fn, 7), "e5m2": (ml_dtypes.float8_e5m2, 14)}[fmt]
    v = np.moveaxis(np.asarray(x, np.float32).astype(ml_dtypes.bfloat16).astype(np.float64), axis, -1)
    blocks = v.reshape(v.shape[:-1] + (-1, 32))
    amax = np.abs(blocks).max(-1, keepdims=True)
    byte = np.maximum(np.where(amax > 0, np.frexp(amax)[1] - 1 + 127, 0) - down, 1)
    scale = np.exp2(byte - 127.0)
    codes = (blocks / scale).astype(np.float32).astype(dtype).astype(np.float64)
    return np.moveaxis((codes * scale).reshape(v.shape), -1, axis)


WIDE = False


def mx_kscale(k):
    if not WIDE:
        return np.ones(k)
    levels = np.array([10, -10, 5, -5, 0])
    a = np.random.permutation(np.resize(levels, k // 512 * 4)).reshape(k // 512, 4)
    idx = np.arange(k)
    return np.exp2(a[idx // 512, idx % 128 // 32])


BF16 = ml_dtypes.bfloat16


def bf(x):
    return np.asarray(x, np.float32).astype(BF16)


def f64(x):
    return np.asarray(x).astype(np.float64)


B, C, GH, GW, F, D, K, T = 24, 1536, 16, 32, 512, 512, 128, 256
N = GH * GW
EPS_NORM = 1e-12
EPS_DENOM = 1e-6


def l2norm(x, axis):
    n = np.sqrt(np.sum(x * x, axis=axis, keepdims=True))
    return x / np.maximum(n, EPS_NORM)


def sigmoid(z):
    return 1.0 / (1.0 + np.exp(-z))


def setup_inputs():
    t = mx_kscale(F)
    c = np.random.standard_normal((B, D))
    g = np.random.standard_normal((B, N))
    f = c[:, :, None] * g[:, None, :] + np.random.standard_normal((B, D, N))
    return {"f_clu": bf(f),
            "h_score": bf(np.maximum(np.random.standard_normal((B, F, N)), 0.0) * t[None, :, None]),
            "W_s2": bf(np.random.standard_normal((K, F)) * 2.5 / np.sqrt(F) / t[None, :]),
            "b_s2": bf(np.random.standard_normal(K) * 0.5),
            "burst_par": bf([5.0 + 0.25 * np.random.standard_normal(),
                             -2.5 + 0.25 * np.random.standard_normal(),
                             0.75 + 0.05 * np.random.standard_normal()])}


def reference(f_clu, h_score, W_s2, b_s2, burst_par):
    f = f64(f_clu)
    a_par, b_par, p_par = f64(burst_par)
    scores = (mxq(f64(W_s2), 1, "e4m3") @ mxq(f64(h_score), 1, "e4m3")) + f64(b_s2)[None, :, None]
    e = np.exp(scores - scores.max(axis=1, keepdims=True))
    alpha = e / e.sum(axis=1, keepdims=True)
    fq = mxq(l2norm(f, 1), 1, "e4m3")
    sim = fq.transpose(0, 2, 1) @ fq
    w = sigmoid(a_par * sim + b_par).sum(axis=2)
    pmat = alpha / (np.power(w, p_par)[:, None, :] + EPS_DENOM)
    v = mxq(f, 2, "e4m3") @ mxq(pmat, 2, "e4m3").transpose(0, 2, 1)
    return l2norm(v, 1)

@@ -1,0 +1,368 @@
+from contextlib import ExitStack
+
+import concourse.mybir as mybir
+from concourse.masks import make_identity
+
+FP8X4 = mybir.dt.float8_e4m3fn_x4
+BF16 = mybir.dt.bfloat16
+F32 = mybir.dt.float32
+U32 = mybir.dt.uint32
+U8 = mybir.dt.uint8
+ACT = mybir.ActivationFunctionType
+ALU = mybir.AluOpType
+AX = mybir.AxisListType
+
+P = 128
+IMAGES = 24
+D = 512
+N = 512
+K = 128
+FLOPS = 2 * IMAGES * (K * 512 * N + N * D * N + D * N * K)
+
+
+def tile_salad_pa_t_kernel(tc, f_clu, h_score, W_s2, b_s2, burst_par, out):
+    nc = tc.nc
+    with ExitStack() as ctx:
+        const = ctx.enter_context(tc.tile_pool(name="const", bufs=1))
+        ld = ctx.enter_context(tc.tile_pool(name="ld", bufs=4))
+        grp = ctx.enter_context(tc.tile_pool(name="grp", bufs=2))
+        qf = ctx.enter_context(tc.tile_pool(name="qf", bufs=4))
+        qs = ctx.enter_context(tc.tile_pool(name="qs", bufs=3))
+        work = ctx.enter_context(tc.tile_pool(name="work", bufs=3))
+        small = ctx.enter_context(tc.tile_pool(name="small", bufs=4))
+        junkp = ctx.enter_context(tc.tile_pool(name="junkp", bufs=1))
+        pft = ctx.enter_context(tc.psum_pool(name="pft", bufs=2))
+        prn = ctx.enter_context(tc.psum_pool(name="prn", bufs=1))
+        psc = ctx.enter_context(tc.psum_pool(name="psc", bufs=1))
+        psim = ctx.enter_context(tc.psum_pool(name="psim", bufs=2))
+        pv = ctx.enter_context(tc.psum_pool(name="pv", bufs=1))
+        paux = ctx.enter_context(tc.psum_pool(name="paux", bufs=1))
+
+        ident = const.tile([P, P], F32, name="ident")
+        make_identity(nc, ident[:])
+        par_bf = const.tile([P, 3], BF16, name="par_bf")
+        nc.sync.dma_start(out=par_bf[:], in_=burst_par.partition_broadcast(P))
+        w_sb = const.tile([P, 512], BF16, name="w_sb")
+        nc.sync.dma_start(out=w_sb[:], in_=W_s2)
+        bias_bf = const.tile([P, K], BF16, name="bias_bf")
+        nc.sync.dma_start(out=bias_bf[:], in_=b_s2.partition_broadcast(P))
+
+        par = const.tile([P, 3], F32, name="par")
+        nc.vector.tensor_copy(out=par[:], in_=par_bf[:])
+        half = const.tile([P, 2], F32, name="half")
+        nc.vector.tensor_scalar_mul(out=half[:], in0=par[:, 0:2], scalar1=0.5)
+        pexp = const.tile([P, 4], F32, name="pexp")
+        nc.vector.tensor_copy(out=pexp[:], in_=par[:, 2:3].to_broadcast([P, 4]))
+        mhalf = const.tile([P, 4], F32, name="mhalf")
+        nc.vector.memset(mhalf[:], -0.5)
+        biasb = const.tile([P, K], F32, name="biasb")
+        nc.vector.tensor_copy(out=biasb[:], in_=bias_bf[:])
+
+        wps = paux.tile([P, 2, P], F32, tag="aux", name="wps")
+        w32 = w_sb[:].bitcast(F32).rearrange("k (p u) -> k p u", u=2)
+        for u in range(2):
+            nc.tensor.transpose(wps[:, u, :], w32[:, :, u], ident[:])
+        g_w = const.tile([P, 4 * K], BF16, name="g_w", align_bytes=64)
+        nc.vector.tensor_copy(
+            out=g_w[:].bitcast(F32).rearrange("p (k u) -> p k u", u=2),
+            in_=wps[:].rearrange("p u k -> p k u"),
+        )
+        w_q = const.tile([P, K], U32, name="w_q", align_bytes=64)
+        w_s = const.tile([P, K], U8, name="w_s", align_bytes=64)
+        nc.vector.quantize_mx(out=w_q[:].bitcast(FP8X4), scales=w_s[:], in_=g_w[:])
+
+        junk_s = junkp.tile([P, 512], BF16, name="junk_s")
+
+        st = {}
+
+        def load(i):
+            f_sb = ld.tile([P, 4 * N], BF16, tag="f", name="f_sb", bufs=4)
+            nc.sync.dma_start(out=f_sb[:], in_=f_clu[i].rearrange("(p j) n -> p (j n)", j=4))
+            h_sb = ld.tile([P, 4 * N], BF16, tag="h", name="h_sb", bufs=3)
+            nc.sync.dma_start(out=h_sb[:], in_=h_score[i].rearrange("(p j) n -> p (j n)", j=4))
+            st[("f", i)] = f_sb
+            st[("h", i)] = h_sb
+
+        def transposes(i):
+            f32v = st[("f", i)][:].bitcast(F32).rearrange("p (j q u) -> p j q u", j=4, u=2)
+            banks = []
+            for b in range(2):
+                ftb = pft.tile([P, 2, 256], F32, tag="ft", name="ftb")
+                for u in range(2):
+                    for jj in range(2):
+                        nc.tensor.transpose(
+                            ftb[:, u, jj * P : (jj + 1) * P], f32v[:, 2 * b + jj, :, u], ident[:]
+                        )
+                banks.append(ftb)
+            st[("ftb", i)] = banks
+
+        def copy_out(i):
+            g_t = grp.tile([P, 4 * D], BF16, tag="gt", name="g_t", align_bytes=64)
+            g_t32 = g_t[:].bitcast(F32).rearrange("q (c u) -> q c u", u=2)
+            for b in range(2):
+                nc.scalar.copy(
+                    out=g_t32[:, b * 256 : (b + 1) * 256, :],
+                    in_=st[("ftb", i)][b][:].rearrange("q u c -> q c u"),
+                )
+            st[("gt", i)] = g_t
+
+        def quant_ft(i):
+            ft_q = qf.tile([P, D], U32, tag="ftq", name="ft_q", align_bytes=64)
+            ft_s = qf.tile([P, D], U8, tag="fts", name="ft_s", align_bytes=64)
+            nc.vector.quantize_mx(out=ft_q[:].bitcast(FP8X4), scales=ft_s[:], in_=st[("gt", i)][:])
+            st[("ftq", i)] = (ft_q, ft_s)
+
+        def squares(i):
+            ss = small.tile([P, 4], F32, tag="ss", name="ss")
+            g_tv = st[("gt", i)][:].rearrange("q (c t) -> q c t", t=4)
+            for t in range(4):
+                nc.scalar.activation(
+                    out=junk_s[:], in_=g_tv[:, :, t], func=ACT.Square, accum_out=ss[:, t : t + 1]
+                )
+            ssm = small.tile([P, 4], F32, tag="ssm", name="ssm")
+            nc.gpsimd.tensor_scalar_max(out=ssm[:], in0=ss[:], scalar1=1e-24)
+            rn = small.tile([P, 4], F32, tag="rn", name="rn")
+            nc.gpsimd.tensor_tensor(out=rn[:], in0=ssm[:], in1=mhalf[:], op=ALU.pow)
+            st[("rn", i)] = rn
+
+        def spread_rn(i):
+            rn = st[("rn", i)]
+            rnb = prn.tile([P, N], F32, tag="rnb", name="rnb")
+            for t in range(4):
+                nc.tensor.transpose(
+                    rnb[:, t * P : (t + 1) * P], rn[:, t : t + 1].to_broadcast([P, P]), ident[:]
+                )
+            st[("rnb", i)] = rnb
+
+        def fn_mult(i):
+            g_f = grp.tile([P, 4 * N], BF16, tag="gf", name="g_f", align_bytes=64)
+            nc.vector.tensor_tensor(
+                out=g_f[:].rearrange("p (t q j) -> p t q j", t=4, j=4),
+                in0=st[("f", i)][:].rearrange("p (j q t) -> p t q j", j=4, t=4),
+                in1=st[("rnb", i)][:]
+                .rearrange("p (t q) -> p t q", t=4)
+                .unsqueeze(3)
+                .to_broadcast([P, 4, P, 4]),
+                op=ALU.mult,
+            )
+            st[("gf", i)] = g_f
+
+        def quant_fn(i):
+            fn_q = qs.tile([P, N], U32, tag="fnq", name="fn_q", align_bytes=64)
+            fn_s = qs.tile([P, N], U8, tag="fns", name="fn_s", align_bytes=64)
+            nc.vector.quantize_mx(out=fn_q[:].bitcast(FP8X4), scales=fn_s[:], in_=st[("gf", i)][:])
+            st[("fnq", i)] = (fn_q, fn_s)
+            st[("ta", i)] = small.tile([P, 4], F32, tag="ta", name="ta")
+
+        def h_regroup(i):
+            g_h = grp.tile([P, 4 * N], BF16, tag="gh", name="g_h", align_bytes=64)
+            nc.vector.tensor_copy(
+                out=g_h[:].rearrange("p (t q j) -> p q j t", t=4, j=4),
+                in_=st[("h", i)][:].rearrange("p (j q t) -> p q j t", j=4, t=4),
+            )
+            st[("gh", i)] = g_h
+
+        def quant_h_scores(i):
+            h_q = qs.tile([P, N], U32, tag="hq", name="h_q", align_bytes=64)
+            h_s = qs.tile([P, N], U8, tag="hs", name="h_s", align_bytes=64)
+            nc.vector.quantize_mx(out=h_q[:].bitcast(FP8X4), scales=h_s[:], in_=st[("gh", i)][:])
+            sc = psc.tile([P, 4 * K], F32, tag="sc", name="sc")
+            for t in range(4):
+                cols = slice(t * P, (t + 1) * P)
+                nc.tensor.matmul_mx(
+                    out=sc[:, cols],
+                    lhsT=h_q[:, cols].bitcast(FP8X4),
+                    lhsT_scale=h_s[:, cols],
+                    rhs=w_q[:].bitcast(FP8X4),
+                    rhs_scale=w_s[:],
+                    start=True,
+                    stop=True,
+                )
+            st[("sc", i)] = sc
+
+        def bias_add(i):
+            sb = work.tile([P, 4 * K], F32, tag="sb", name="sb")
+            nc.vector.tensor_tensor(
+                out=sb[:].rearrange("q (t k) -> q t k", t=4),
+                in0=st[("sc", i)][:].rearrange("q (t k) -> q t k", t=4),
+                in1=biasb[:].unsqueeze(1).to_broadcast([P, 4, K]),
+                op=ALU.add,
+            )
+            st[("sb", i)] = sb
+
+        def row_max(i):
+            nm = small.tile([P, 4], F32, tag="nm", name="nm")
+            nc.vector.tensor_reduce(
+                out=nm[:],
+                in_=st[("sb", i)][:].rearrange("q (t k) -> q t k", t=4),
+                axis=AX.X,
+                op=ALU.max,
+                negate=True,
+            )
+            st[("nm", i)] = nm
+
+        def exps(i):
+            sb = st[("sb", i)]
+            nm = st[("nm", i)]
+            e = work.tile([P, 4 * K], F32, tag="e", name="e")
+            se = small.tile([P, 4], F32, tag="se", name="se")
+            for t in range(4):
+                cols = slice(t * K, (t + 1) * K)
+                nc.scalar.activation(
+                    out=e[:, cols],
+                    in_=sb[:, cols],
+                    func=ACT.Exp,
+                    bias=nm[:, t : t + 1],
+                    scale=1.0,
+                    accum_out=se[:, t : t + 1],
+                )
+            st[("e", i)] = (e, se)
+
+        def sim(i, t):
+            fn_q, fn_s = st[("fnq", i)]
+            cols = slice(t * P, (t + 1) * P)
+            sm = psim.tile([P, N], F32, tag="sim", name="sm")
+            nc.tensor.matmul_mx(
+                out=sm[:],
+                lhsT=fn_q[:, cols].bitcast(FP8X4),
+                lhsT_scale=fn_s[:, cols],
+                rhs=fn_q[:].bitcast(FP8X4),
+                rhs_scale=fn_s[:],
+                start=True,
+                stop=True,
+            )
+            st[("sm", i, t)] = sm
+
+        def tanh(i, t):
+            nc.scalar.activation(
+                out=junk_s[:],
+                in_=st[("sm", i, t)][:],
+                func=ACT.Tanh,
+                bias=half[:, 1:2],
+                scale=half[:, 0:1],
+                accum_out=st[("ta", i)][:, t : t + 1],
+            )
+
+        def burst(i):
+            w = small.tile([P, 4], F32, tag="w", name="w")
+            nc.gpsimd.tensor_scalar(
+                out=w[:], in0=st[("ta", i)][:], scalar1=0.5, scalar2=0.5 * N, op0=ALU.mult, op1=ALU.add
+            )
+            wp = small.tile([P, 4], F32, tag="wp", name="wp")
+            nc.gpsimd.tensor_tensor(out=wp[:], in0=w[:], in1=pexp[:], op=ALU.pow)
+            wpe = small.tile([P, 4], F32, tag="wpe", name="wpe")
+            nc.gpsimd.tensor_scalar_add(out=wpe[:], in0=wp[:], scalar1=1e-6)
+            st[("wpe", i)] = wpe
+
+        def pmat(i):
+            e, se = st[("e", i)]
+            den = small.tile([P, 4], F32, tag="den", name="den")
+            nc.vector.tensor_tensor(out=den[:], in0=st[("wpe", i)][:], in1=se[:], op=ALU.mult)
+            c = small.tile([P, 4], F32, tag="c", name="c")
+            nc.vector.reciprocal(out=c[:], in_=den[:])
+            g_p = grp.tile([P, 4 * K], BF16, tag="gp", name="g_p", align_bytes=64)
+            nc.vector.tensor_tensor(
+                out=g_p[:].rearrange("q (k t) -> q k t", t=4),
+                in0=e[:].rearrange("q (t k) -> q k t", t=4),
+                in1=c[:].unsqueeze(1).to_broadcast([P, K, 4]),
+                op=ALU.mult,
+            )
+            st[("gp", i)] = g_p
+
+        def quant_p_vt(i):
+            ft_q, ft_s = st[("ftq", i)]
+            p_q = qs.tile([P, K], U32, tag="pq", name="p_q", align_bytes=64)
+            p_s = qs.tile([P, K], U8, tag="ps", name="p_s", align_bytes=64)
+            nc.vector.quantize_mx(out=p_q[:].bitcast(FP8X4), scales=p_s[:], in_=st[("gp", i)][:])
+            vt = paux.tile([P, D], F32, tag="aux", name="vt")
+            nc.tensor.matmul_mx(
+                out=vt[:],
+                lhsT=p_q[:].bitcast(FP8X4),
+                lhsT_scale=p_s[:],
+                rhs=ft_q[:].bitcast(FP8X4),
+                rhs_scale=ft_s[:],
+                start=True,
+                stop=True,
+            )
+            st[("pq", i)] = (p_q, p_s)
+            st[("vt", i)] = vt
+
+        def square_vt(i):
+            sv = small.tile([P, 1], F32, tag="sv", name="sv")
+            nc.scalar.activation(out=junk_s[:], in_=st[("vt", i)][:], func=ACT.Square, accum_out=sv[:])
+            svm = small.tile([P, 1], F32, tag="svm", name="svm")
+            nc.gpsimd.tensor_scalar_max(out=svm[:], in0=sv[:], scalar1=1e-24)
+            rv = small.tile([P, 1], F32, tag="rv", name="rv")
+            nc.gpsimd.tensor_tensor(out=rv[:], in0=svm[:], in1=mhalf[:, 0:1], op=ALU.pow)
+            st[("rv", i)] = rv
+
+        def spread_rv_v(i):
+            ft_q, ft_s = st[("ftq", i)]
+            p_q, p_s = st[("pq", i)]
+            rvp = paux.tile([P, K], F32, tag="aux", name="rvp")
+            nc.tensor.transpose(rvp[:], st[("rv", i)][:, 0:1].to_broadcast([P, P]), ident[:])
+            v = pv.tile([P, 4 * K], F32, tag="v", name="v")
+            for j in range(4):
+                cols = slice(j * P, (j + 1) * P)
+                nc.tensor.matmul_mx(
+                    out=v[:, j * K : (j + 1) * K],
+                    lhsT=ft_q[:, cols].bitcast(FP8X4),
+                    lhsT_scale=ft_s[:, cols],
+                    rhs=p_q[:].bitcast(FP8X4),
+                    rhs_scale=p_s[:],
+                    start=True,
+                    stop=True,
+                )
+            st[("rvp", i)] = rvp
+            st[("v", i)] = v
+
+        def copy_rv(i):
+            rvs = work.tile([P, K], F32, tag="rvs", name="rvs")
+            nc.scalar.copy(out=rvs[:], in_=st[("rvp", i)][:])
+            st[("rvs", i)] = rvs
+
+        def final(i):
+            o = work.tile([P, 4 * K], F32, tag="o", name="o")
+            nc.vector.tensor_tensor(
+                out=o[:].rearrange("p (j k) -> p j k", j=4),
+                in0=st[("v", i)][:].rearrange("p (j k) -> p j k", j=4),
+                in1=st[("rvs", i)][:].unsqueeze(1).to_broadcast([P, 4, K]),
+                op=ALU.mult,
+            )
+            nc.sync.dma_start(out=out[i].rearrange("(p j) k -> p (j k)", j=4), in_=o[:])
+
+        def on(step, i, *args):
+            if 0 <= i < IMAGES:
+                step(i, *args)
+
+        load(0)
+        with tc.manual_schedule():
+            for r in range(-1, IMAGES + 3):
+                on(load, r + 2)
+                on(fn_mult, r - 1)
+                on(copy_out, r)
+                on(square_vt, r - 3)
+                on(quant_ft, r)
+                on(squares, r)
+                on(quant_fn, r - 1)
+                on(sim, r - 1, 0)
+                on(sim, r - 1, 1)
+                on(h_regroup, r)
+                on(exps, r - 2)
+                on(spread_rv_v, r - 3)
+                on(copy_rv, r - 3)
+                on(tanh, r - 1, 0)
+                on(sim, r - 1, 2)
+                on(tanh, r - 1, 1)
+                on(sim, r - 1, 3)
+                on(tanh, r - 1, 2)
+                on(tanh, r - 1, 3)
+                on(burst, r - 1)
+                on(bias_add, r - 1)
+                on(quant_h_scores, r)
+                on(row_max, r - 1)
+                on(spread_rn, r)
+                on(pmat, r - 2)
+                on(transposes, r + 1)
+                on(final, r - 3)
+                on(quant_p_vt, r - 2)

@@ -26,7 +26,7 @@ def tile_salad_pa_t_kernel(tc, f_clu, h_score, W_s2, b_s2, burst_par, out):
         const = ctx.enter_context(tc.tile_pool(name="const", bufs=1))
         ld = ctx.enter_context(tc.tile_pool(name="ld", bufs=4))
         grp = ctx.enter_context(tc.tile_pool(name="grp", bufs=2))
-        qf = ctx.enter_context(tc.tile_pool(name="qf", bufs=4))
+        qf = ctx.enter_context(tc.tile_pool(name="qf", bufs=5))
         qs = ctx.enter_context(tc.tile_pool(name="qs", bufs=3))
         work = ctx.enter_context(tc.tile_pool(name="work", bufs=3))
         small = ctx.enter_context(tc.tile_pool(name="small", bufs=4))
@@ -162,10 +162,14 @@ def tile_salad_pa_t_kernel(tc, f_clu, h_score, W_s2, b_s2, burst_par, out):
             )
             st[("gh", i)] = g_h
 
-        def quant_h_scores(i):
+        def quant_h(i):
             h_q = qs.tile([P, N], U32, tag="hq", name="h_q", align_bytes=64)
             h_s = qs.tile([P, N], U8, tag="hs", name="h_s", align_bytes=64)
             nc.vector.quantize_mx(out=h_q[:].bitcast(FP8X4), scales=h_s[:], in_=st[("gh", i)][:])
+            st[("hq", i)] = (h_q, h_s)
+
+        def scores(i):
+            h_q, h_s = st[("hq", i)]
             sc = psc.tile([P, 4 * K], F32, tag="sc", name="sc")
             for t in range(4):
                 cols = slice(t * P, (t + 1) * P)
@@ -269,11 +273,15 @@ def tile_salad_pa_t_kernel(tc, f_clu, h_score, W_s2, b_s2, burst_par, out):
             )
             st[("gp", i)] = g_p
 
-        def quant_p_vt(i):
-            ft_q, ft_s = st[("ftq", i)]
+        def quant_p(i):
             p_q = qs.tile([P, K], U32, tag="pq", name="p_q", align_bytes=64)
             p_s = qs.tile([P, K], U8, tag="ps", name="p_s", align_bytes=64)
             nc.vector.quantize_mx(out=p_q[:].bitcast(FP8X4), scales=p_s[:], in_=st[("gp", i)][:])
+            st[("pq", i)] = (p_q, p_s)
+
+        def v_transposed(i):
+            ft_q, ft_s = st[("ftq", i)]
+            p_q, p_s = st[("pq", i)]
             vt = paux.tile([P, D], F32, tag="aux", name="vt")
             nc.tensor.matmul_mx(
                 out=vt[:],
@@ -284,7 +292,6 @@ def tile_salad_pa_t_kernel(tc, f_clu, h_score, W_s2, b_s2, burst_par, out):
                 start=True,
                 stop=True,
             )
-            st[("pq", i)] = (p_q, p_s)
             st[("vt", i)] = vt
 
         def square_vt(i):
@@ -296,11 +303,14 @@ def tile_salad_pa_t_kernel(tc, f_clu, h_score, W_s2, b_s2, burst_par, out):
             nc.gpsimd.tensor_tensor(out=rv[:], in0=svm[:], in1=mhalf[:, 0:1], op=ALU.pow)
             st[("rv", i)] = rv
 
-        def spread_rv_v(i):
-            ft_q, ft_s = st[("ftq", i)]
-            p_q, p_s = st[("pq", i)]
+        def spread_rv(i):
             rvp = paux.tile([P, K], F32, tag="aux", name="rvp")
             nc.tensor.transpose(rvp[:], st[("rv", i)][:, 0:1].to_broadcast([P, P]), ident[:])
+            st[("rvp", i)] = rvp
+
+        def v_rows(i):
+            ft_q, ft_s = st[("ftq", i)]
+            p_q, p_s = st[("pq", i)]
             v = pv.tile([P, 4 * K], F32, tag="v", name="v")
             for j in range(4):
                 cols = slice(j * P, (j + 1) * P)
@@ -313,7 +323,6 @@ def tile_salad_pa_t_kernel(tc, f_clu, h_score, W_s2, b_s2, burst_par, out):
                     start=True,
                     stop=True,
                 )
-            st[("rvp", i)] = rvp
             st[("v", i)] = v
 
         def copy_rv(i):
@@ -337,32 +346,35 @@ def tile_salad_pa_t_kernel(tc, f_clu, h_score, W_s2, b_s2, burst_par, out):
 
         load(0)
         with tc.manual_schedule():
-            for r in range(-1, IMAGES + 3):
+            for r in range(-1, IMAGES + 5):
                 on(load, r + 2)
-                on(fn_mult, r - 1)
+                on(scores, r - 1)
                 on(copy_out, r)
-                on(square_vt, r - 3)
-                on(quant_ft, r)
-                on(squares, r)
-                on(quant_fn, r - 1)
-                on(sim, r - 1, 0)
-                on(sim, r - 1, 1)
                 on(h_regroup, r)
-                on(exps, r - 2)
-                on(spread_rv_v, r - 3)
-                on(copy_rv, r - 3)
-                on(tanh, r - 1, 0)
-                on(sim, r - 1, 2)
-                on(tanh, r - 1, 1)
-                on(sim, r - 1, 3)
-                on(tanh, r - 1, 2)
-                on(tanh, r - 1, 3)
-                on(burst, r - 1)
-                on(bias_add, r - 1)
-                on(quant_h_scores, r)
-                on(row_max, r - 1)
-                on(spread_rn, r)
-                on(pmat, r - 2)
+                on(sim, r - 2, 0)
+                on(sim, r - 2, 1)
+                on(pmat, r - 3)
+                on(squares, r)
+                on(quant_h, r)
+                on(quant_p, r - 3)
+                on(spread_rn, r - 1)
                 on(transposes, r + 1)
-                on(final, r - 3)
-                on(quant_p_vt, r - 2)
+                on(spread_rv, r - 4)
+                on(v_rows, r - 4)
+                on(bias_add, r - 1)
+                on(quant_ft, r)
+                on(row_max, r - 1)
+                on(tanh, r - 2, 0)
+                on(tanh, r - 2, 1)
+                on(copy_rv, r - 4)
+                on(sim, r - 2, 2)
+                on(sim, r - 2, 3)
+                on(v_transposed, r - 3)
+                on(exps, r - 2)
+                on(fn_mult, r - 1)
+                on(tanh, r - 2, 2)
+                on(tanh, r - 2, 3)
+                on(burst, r - 2)
+                on(square_vt, r - 3)
+                on(final, r - 4)
+                on(quant_fn, r - 1)

@@ -157,8 +157,8 @@ def tile_salad_pa_t_kernel(tc, f_clu, h_score, W_s2, b_s2, burst_par, out):
         def h_regroup(i):
             g_h = grp.tile([P, 4 * N], BF16, tag="gh", name="g_h", align_bytes=64)
             nc.vector.tensor_copy(
-                out=g_h[:].rearrange("p (t q j) -> p q j t", t=4, j=4),
-                in_=st[("h", i)][:].rearrange("p (j q t) -> p q j t", j=4, t=4),
+                out=g_h[:].rearrange("p (t q j) -> p t q j", t=4, j=4),
+                in_=st[("h", i)][:].rearrange("p (j q t) -> p t q j", j=4, t=4),
             )
             st[("gh", i)] = g_h
 

@@ -26,7 +26,7 @@ def tile_salad_pa_t_kernel(tc, f_clu, h_score, W_s2, b_s2, burst_par, out):
         const = ctx.enter_context(tc.tile_pool(name="const", bufs=1))
         ld = ctx.enter_context(tc.tile_pool(name="ld", bufs=4))
         grp = ctx.enter_context(tc.tile_pool(name="grp", bufs=2))
-        qf = ctx.enter_context(tc.tile_pool(name="qf", bufs=5))
+        qf = ctx.enter_context(tc.tile_pool(name="qf", bufs=7))
         qs = ctx.enter_context(tc.tile_pool(name="qs", bufs=3))
         work = ctx.enter_context(tc.tile_pool(name="work", bufs=3))
         small = ctx.enter_context(tc.tile_pool(name="small", bufs=4))
@@ -51,10 +51,9 @@ def tile_salad_pa_t_kernel(tc, f_clu, h_score, W_s2, b_s2, burst_par, out):
         nc.vector.tensor_copy(out=par[:], in_=par_bf[:])
         half = const.tile([P, 2], F32, name="half")
         nc.vector.tensor_scalar_mul(out=half[:], in0=par[:, 0:2], scalar1=0.5)
-        pexp = const.tile([P, 4], F32, name="pexp")
-        nc.vector.tensor_copy(out=pexp[:], in_=par[:, 2:3].to_broadcast([P, 4]))
-        mhalf = const.tile([P, 4], F32, name="mhalf")
-        nc.vector.memset(mhalf[:], -0.5)
+        expo = const.tile([P, 9], F32, name="expo")
+        nc.vector.memset(expo[:], -0.5)
+        nc.vector.tensor_copy(out=expo[:, 4:8], in_=par[:, 2:3].to_broadcast([P, 4]))
         biasb = const.tile([P, K], F32, name="biasb")
         nc.vector.tensor_copy(out=biasb[:], in_=bias_bf[:])
 
@@ -76,7 +75,7 @@ def tile_salad_pa_t_kernel(tc, f_clu, h_score, W_s2, b_s2, burst_par, out):
         st = {}
 
         def load(i):
-            f_sb = ld.tile([P, 4 * N], BF16, tag="f", name="f_sb", bufs=4)
+            f_sb = ld.tile([P, 4 * N], BF16, tag="f", name="f_sb", bufs=5)
             nc.sync.dma_start(out=f_sb[:], in_=f_clu[i].rearrange("(p j) n -> p (j n)", j=4))
             h_sb = ld.tile([P, 4 * N], BF16, tag="h", name="h_sb", bufs=3)
             nc.sync.dma_start(out=h_sb[:], in_=h_score[i].rearrange("(p j) n -> p (j n)", j=4))
@@ -112,21 +111,16 @@ def tile_salad_pa_t_kernel(tc, f_clu, h_score, W_s2, b_s2, burst_par, out):
             nc.vector.quantize_mx(out=ft_q[:].bitcast(FP8X4), scales=ft_s[:], in_=st[("gt", i)][:])
             st[("ftq", i)] = (ft_q, ft_s)
 
-        def squares(i):
-            ss = small.tile([P, 4], F32, tag="ss", name="ss")
-            g_tv = st[("gt", i)][:].rearrange("q (c t) -> q c t", t=4)
-            for t in range(4):
-                nc.scalar.activation(
-                    out=junk_s[:], in_=g_tv[:, :, t], func=ACT.Square, accum_out=ss[:, t : t + 1]
-                )
-            ssm = small.tile([P, 4], F32, tag="ssm", name="ssm")
-            nc.gpsimd.tensor_scalar_max(out=ssm[:], in0=ss[:], scalar1=1e-24)
-            rn = small.tile([P, 4], F32, tag="rn", name="rn")
-            nc.gpsimd.tensor_tensor(out=rn[:], in0=ssm[:], in1=mhalf[:], op=ALU.pow)
-            st[("rn", i)] = rn
+        def square(i, t):
+            nc.scalar.activation(
+                out=junk_s[:],
+                in_=st[("gt", i)][:].rearrange("q (c t) -> q c t", t=4)[:, :, t],
+                func=ACT.Square,
+                accum_out=st[("x", i)][:, t : t + 1],
+            )
 
         def spread_rn(i):
-            rn = st[("rn", i)]
+            rn = st[("y", i)]
             rnb = prn.tile([P, N], F32, tag="rnb", name="rnb")
             for t in range(4):
                 nc.tensor.transpose(
@@ -152,13 +146,12 @@ def tile_salad_pa_t_kernel(tc, f_clu, h_score, W_s2, b_s2, burst_par, out):
             fn_s = qs.tile([P, N], U8, tag="fns", name="fn_s", align_bytes=64)
             nc.vector.quantize_mx(out=fn_q[:].bitcast(FP8X4), scales=fn_s[:], in_=st[("gf", i)][:])
             st[("fnq", i)] = (fn_q, fn_s)
-            st[("ta", i)] = small.tile([P, 4], F32, tag="ta", name="ta")
 
         def h_regroup(i):
             g_h = grp.tile([P, 4 * N], BF16, tag="gh", name="g_h", align_bytes=64)
             nc.vector.tensor_copy(
-                out=g_h[:].rearrange("p (t q j) -> p t q j", t=4, j=4),
-                in_=st[("h", i)][:].rearrange("p (j q t) -> p t q j", j=4, t=4),
+                out=g_h[:].rearrange("p (t q j) -> p q j t", t=4, j=4),
+                in_=st[("h", i)][:].rearrange("p (j q t) -> p q j t", j=4, t=4),
             )
             st[("gh", i)] = g_h
 
@@ -244,24 +237,35 @@ def tile_salad_pa_t_kernel(tc, f_clu, h_score, W_s2, b_s2, burst_par, out):
                 func=ACT.Tanh,
                 bias=half[:, 1:2],
                 scale=half[:, 0:1],
-                accum_out=st[("ta", i)][:, t : t + 1],
+                accum_out=st[("x", i + 3)][:, 4 + t : 5 + t],
             )
 
-        def burst(i):
-            w = small.tile([P, 4], F32, tag="w", name="w")
-            nc.gpsimd.tensor_scalar(
-                out=w[:], in0=st[("ta", i)][:], scalar1=0.5, scalar2=0.5 * N, op0=ALU.mult, op1=ALU.add
-            )
-            wp = small.tile([P, 4], F32, tag="wp", name="wp")
-            nc.gpsimd.tensor_tensor(out=wp[:], in0=w[:], in1=pexp[:], op=ALU.pow)
-            wpe = small.tile([P, 4], F32, tag="wpe", name="wpe")
-            nc.gpsimd.tensor_scalar_add(out=wpe[:], in0=wp[:], scalar1=1e-6)
-            st[("wpe", i)] = wpe
+        def powers(r):
+            has_f = 0 <= r < IMAGES
+            has_w = 0 <= r - 3 < IMAGES
+            has_v = 0 <= r - 5 < IMAGES
+            x = st[("x", r)]
+            m = small.tile([P, 9], F32, tag="m", name="m")
+            y = small.tile([P, 9], F32, tag="y", name="y")
+            if has_f:
+                nc.gpsimd.tensor_scalar_max(out=m[:, 0:4], in0=x[:, 0:4], scalar1=1e-24)
+            if has_w:
+                nc.gpsimd.tensor_scalar(
+                    out=m[:, 4:8], in0=x[:, 4:8], scalar1=0.5, scalar2=0.5 * N, op0=ALU.mult, op1=ALU.add
+                )
+            if has_v:
+                nc.gpsimd.tensor_scalar_max(out=m[:, 8:9], in0=x[:, 8:9], scalar1=1e-24)
+            lo = 0 if has_f else (4 if has_w else 8)
+            hi = 9 if has_v else (8 if has_w else 4)
+            nc.gpsimd.tensor_tensor(out=y[:, lo:hi], in0=m[:, lo:hi], in1=expo[:, lo:hi], op=ALU.pow)
+            if has_w:
+                nc.gpsimd.tensor_scalar_add(out=y[:, 4:8], in0=y[:, 4:8], scalar1=1e-6)
+            st[("y", r)] = y
 
         def pmat(i):
             e, se = st[("e", i)]
             den = small.tile([P, 4], F32, tag="den", name="den")
-            nc.vector.tensor_tensor(out=den[:], in0=st[("wpe", i)][:], in1=se[:], op=ALU.mult)
+            nc.vector.tensor_tensor(out=den[:], in0=st[("y", i + 3)][:, 4:8], in1=se[:], op=ALU.mult)
             c = small.tile([P, 4], F32, tag="c", name="c")
             nc.vector.reciprocal(out=c[:], in_=den[:])
             g_p = grp.tile([P, 4 * K], BF16, tag="gp", name="g_p", align_bytes=64)
@@ -295,17 +299,13 @@ def tile_salad_pa_t_kernel(tc, f_clu, h_score, W_s2, b_s2, burst_par, out):
             st[("vt", i)] = vt
 
         def square_vt(i):
-            sv = small.tile([P, 1], F32, tag="sv", name="sv")
-            nc.scalar.activation(out=junk_s[:], in_=st[("vt", i)][:], func=ACT.Square, accum_out=sv[:])
-            svm = small.tile([P, 1], F32, tag="svm", name="svm")
-            nc.gpsimd.tensor_scalar_max(out=svm[:], in0=sv[:], scalar1=1e-24)
-            rv = small.tile([P, 1], F32, tag="rv", name="rv")
-            nc.gpsimd.tensor_tensor(out=rv[:], in0=svm[:], in1=mhalf[:, 0:1], op=ALU.pow)
-            st[("rv", i)] = rv
+            nc.scalar.activation(
+                out=junk_s[:], in_=st[("vt", i)][:], func=ACT.Square, accum_out=st[("x", i + 5)][:, 8:9]
+            )
 
         def spread_rv(i):
             rvp = paux.tile([P, K], F32, tag="aux", name="rvp")
-            nc.tensor.transpose(rvp[:], st[("rv", i)][:, 0:1].to_broadcast([P, P]), ident[:])
+            nc.tensor.transpose(rvp[:], st[("y", i + 5)][:, 8:9].to_broadcast([P, P]), ident[:])
             st[("rvp", i)] = rvp
 
         def v_rows(i):
@@ -346,35 +346,41 @@ def tile_salad_pa_t_kernel(tc, f_clu, h_score, W_s2, b_s2, burst_par, out):
 
         load(0)
         with tc.manual_schedule():
-            for r in range(-1, IMAGES + 5):
+            for r in range(-1, IMAGES + 7):
                 on(load, r + 2)
+                if 0 <= r < IMAGES + 5:
+                    st[("x", r)] = small.tile([P, 9], F32, tag="x", name="x")
                 on(scores, r - 1)
                 on(copy_out, r)
+                on(square_vt, r - 5)
+                on(fn_mult, r - 2)
+                on(tanh, r - 3, 0)
+                on(square, r, 0)
+                on(sim, r - 3, 2)
+                on(tanh, r - 3, 1)
+                on(square, r, 1)
+                on(sim, r - 3, 3)
+                on(transposes, r + 1)
                 on(h_regroup, r)
+                on(quant_ft, r)
+                on(quant_h, r)
+                on(tanh, r - 3, 2)
+                on(square, r, 2)
+                on(tanh, r - 3, 3)
+                on(square, r, 3)
+                on(spread_rn, r - 1)
+                on(spread_rv, r - 6)
+                on(v_rows, r - 6)
+                on(pmat, r - 4)
+                on(quant_fn, r - 2)
+                on(quant_p, r - 4)
+                on(exps, r - 2)
+                on(copy_rv, r - 6)
+                if 0 <= r < IMAGES + 5:
+                    powers(r)
+                on(v_transposed, r - 4)
                 on(sim, r - 2, 0)
                 on(sim, r - 2, 1)
-                on(pmat, r - 3)
-                on(squares, r)
-                on(quant_h, r)
-                on(quant_p, r - 3)
-                on(spread_rn, r - 1)
-                on(transposes, r + 1)
-                on(spread_rv, r - 4)
-                on(v_rows, r - 4)
                 on(bias_add, r - 1)
-                on(quant_ft, r)
                 on(row_max, r - 1)
-                on(tanh, r - 2, 0)
-                on(tanh, r - 2, 1)
-                on(copy_rv, r - 4)
-                on(sim, r - 2, 2)
-                on(sim, r - 2, 3)
-                on(v_transposed, r - 3)
-                on(exps, r - 2)
-                on(fn_mult, r - 1)
-                on(tanh, r - 2, 2)
-                on(tanh, r - 2, 3)
-                on(burst, r - 2)
-                on(square_vt, r - 3)
-                on(final, r - 4)
-                on(quant_fn, r - 1)
+                on(final, r - 6)

@@ -26,7 +26,7 @@ def tile_salad_pa_t_kernel(tc, f_clu, h_score, W_s2, b_s2, burst_par, out):
         const = ctx.enter_context(tc.tile_pool(name="const", bufs=1))
         ld = ctx.enter_context(tc.tile_pool(name="ld", bufs=4))
         grp = ctx.enter_context(tc.tile_pool(name="grp", bufs=2))
-        qf = ctx.enter_context(tc.tile_pool(name="qf", bufs=7))
+        qf = ctx.enter_context(tc.tile_pool(name="qf", bufs=5))
         qs = ctx.enter_context(tc.tile_pool(name="qs", bufs=3))
         work = ctx.enter_context(tc.tile_pool(name="work", bufs=3))
         small = ctx.enter_context(tc.tile_pool(name="small", bufs=4))
@@ -51,9 +51,10 @@ def tile_salad_pa_t_kernel(tc, f_clu, h_score, W_s2, b_s2, burst_par, out):
         nc.vector.tensor_copy(out=par[:], in_=par_bf[:])
         half = const.tile([P, 2], F32, name="half")
         nc.vector.tensor_scalar_mul(out=half[:], in0=par[:, 0:2], scalar1=0.5)
-        expo = const.tile([P, 9], F32, name="expo")
-        nc.vector.memset(expo[:], -0.5)
-        nc.vector.tensor_copy(out=expo[:, 4:8], in_=par[:, 2:3].to_broadcast([P, 4]))
+        pexp = const.tile([P, 4], F32, name="pexp")
+        nc.vector.tensor_copy(out=pexp[:], in_=par[:, 2:3].to_broadcast([P, 4]))
+        mhalf = const.tile([P, 4], F32, name="mhalf")
+        nc.vector.memset(mhalf[:], -0.5)
         biasb = const.tile([P, K], F32, name="biasb")
         nc.vector.tensor_copy(out=biasb[:], in_=bias_bf[:])
 
@@ -75,7 +76,7 @@ def tile_salad_pa_t_kernel(tc, f_clu, h_score, W_s2, b_s2, burst_par, out):
         st = {}
 
         def load(i):
-            f_sb = ld.tile([P, 4 * N], BF16, tag="f", name="f_sb", bufs=5)
+            f_sb = ld.tile([P, 4 * N], BF16, tag="f", name="f_sb", bufs=4)
             nc.sync.dma_start(out=f_sb[:], in_=f_clu[i].rearrange("(p j) n -> p (j n)", j=4))
             h_sb = ld.tile([P, 4 * N], BF16, tag="h", name="h_sb", bufs=3)
             nc.sync.dma_start(out=h_sb[:], in_=h_score[i].rearrange("(p j) n -> p (j n)", j=4))
@@ -111,16 +112,21 @@ def tile_salad_pa_t_kernel(tc, f_clu, h_score, W_s2, b_s2, burst_par, out):
             nc.vector.quantize_mx(out=ft_q[:].bitcast(FP8X4), scales=ft_s[:], in_=st[("gt", i)][:])
             st[("ftq", i)] = (ft_q, ft_s)
 
-        def square(i, t):
-            nc.scalar.activation(
-                out=junk_s[:],
-                in_=st[("gt", i)][:].rearrange("q (c t) -> q c t", t=4)[:, :, t],
-                func=ACT.Square,
-                accum_out=st[("x", i)][:, t : t + 1],
-            )
+        def squares(i):
+            ss = small.tile([P, 4], F32, tag="ss", name="ss")
+            g_tv = st[("gt", i)][:].rearrange("q (c t) -> q c t", t=4)
+            for t in range(4):
+                nc.scalar.activation(
+                    out=junk_s[:], in_=g_tv[:, :, t], func=ACT.Square, accum_out=ss[:, t : t + 1]
+                )
+            ssm = small.tile([P, 4], F32, tag="ssm", name="ssm")
+            nc.gpsimd.tensor_scalar_max(out=ssm[:], in0=ss[:], scalar1=1e-24)
+            rn = small.tile([P, 4], F32, tag="rn", name="rn")
+            nc.gpsimd.tensor_tensor(out=rn[:], in0=ssm[:], in1=mhalf[:], op=ALU.pow)
+            st[("rn", i)] = rn
 
         def spread_rn(i):
-            rn = st[("y", i)]
+            rn = st[("rn", i)]
             rnb = prn.tile([P, N], F32, tag="rnb", name="rnb")
             for t in range(4):
                 nc.tensor.transpose(
@@ -131,12 +137,12 @@ def tile_salad_pa_t_kernel(tc, f_clu, h_score, W_s2, b_s2, burst_par, out):
         def fn_mult(i):
             g_f = grp.tile([P, 4 * N], BF16, tag="gf", name="g_f", align_bytes=64)
             nc.vector.tensor_tensor(
-                out=g_f[:].rearrange("p (t q j) -> p t q j", t=4, j=4),
-                in0=st[("f", i)][:].rearrange("p (j q t) -> p t q j", j=4, t=4),
+                out=g_f[:].rearrange("p (t q j) -> p q j t", t=4, j=4),
+                in0=st[("f", i)][:].rearrange("p (j q t) -> p q j t", j=4, t=4),
                 in1=st[("rnb", i)][:]
-                .rearrange("p (t q) -> p t q", t=4)
-                .unsqueeze(3)
-                .to_broadcast([P, 4, P, 4]),
+                .rearrange("p (t q) -> p q t", t=4)
+                .unsqueeze(2)
+                .to_broadcast([P, P, 4, 4]),
                 op=ALU.mult,
             )
             st[("gf", i)] = g_f
@@ -146,6 +152,7 @@ def tile_salad_pa_t_kernel(tc, f_clu, h_score, W_s2, b_s2, burst_par, out):
             fn_s = qs.tile([P, N], U8, tag="fns", name="fn_s", align_bytes=64)
             nc.vector.quantize_mx(out=fn_q[:].bitcast(FP8X4), scales=fn_s[:], in_=st[("gf", i)][:])
             st[("fnq", i)] = (fn_q, fn_s)
+            st[("ta", i)] = small.tile([P, 4], F32, tag="ta", name="ta")
 
         def h_regroup(i):
             g_h = grp.tile([P, 4 * N], BF16, tag="gh", name="g_h", align_bytes=64)
@@ -237,35 +244,24 @@ def tile_salad_pa_t_kernel(tc, f_clu, h_score, W_s2, b_s2, burst_par, out):
                 func=ACT.Tanh,
                 bias=half[:, 1:2],
                 scale=half[:, 0:1],
-                accum_out=st[("x", i + 3)][:, 4 + t : 5 + t],
+                accum_out=st[("ta", i)][:, t : t + 1],
             )
 
-        def powers(r):
-            has_f = 0 <= r < IMAGES
-            has_w = 0 <= r - 3 < IMAGES
-            has_v = 0 <= r - 5 < IMAGES
-            x = st[("x", r)]
-            m = small.tile([P, 9], F32, tag="m", name="m")
-            y = small.tile([P, 9], F32, tag="y", name="y")
-            if has_f:
-                nc.gpsimd.tensor_scalar_max(out=m[:, 0:4], in0=x[:, 0:4], scalar1=1e-24)
-            if has_w:
-                nc.gpsimd.tensor_scalar(
-                    out=m[:, 4:8], in0=x[:, 4:8], scalar1=0.5, scalar2=0.5 * N, op0=ALU.mult, op1=ALU.add
-                )
-            if has_v:
-                nc.gpsimd.tensor_scalar_max(out=m[:, 8:9], in0=x[:, 8:9], scalar1=1e-24)
-            lo = 0 if has_f else (4 if has_w else 8)
-            hi = 9 if has_v else (8 if has_w else 4)
-            nc.gpsimd.tensor_tensor(out=y[:, lo:hi], in0=m[:, lo:hi], in1=expo[:, lo:hi], op=ALU.pow)
-            if has_w:
-                nc.gpsimd.tensor_scalar_add(out=y[:, 4:8], in0=y[:, 4:8], scalar1=1e-6)
-            st[("y", r)] = y
+        def burst(i):
+            w = small.tile([P, 4], F32, tag="w", name="w")
+            nc.gpsimd.tensor_scalar(
+                out=w[:], in0=st[("ta", i)][:], scalar1=0.5, scalar2=0.5 * N, op0=ALU.mult, op1=ALU.add
+            )
+            wp = small.tile([P, 4], F32, tag="wp", name="wp")
+            nc.gpsimd.tensor_tensor(out=wp[:], in0=w[:], in1=pexp[:], op=ALU.pow)
+            wpe = small.tile([P, 4], F32, tag="wpe", name="wpe")
+            nc.gpsimd.tensor_scalar_add(out=wpe[:], in0=wp[:], scalar1=1e-6)
+            st[("wpe", i)] = wpe
 
         def pmat(i):
             e, se = st[("e", i)]
             den = small.tile([P, 4], F32, tag="den", name="den")
-            nc.vector.tensor_tensor(out=den[:], in0=st[("y", i + 3)][:, 4:8], in1=se[:], op=ALU.mult)
+            nc.vector.tensor_tensor(out=den[:], in0=st[("wpe", i)][:], in1=se[:], op=ALU.mult)
             c = small.tile([P, 4], F32, tag="c", name="c")
             nc.vector.reciprocal(out=c[:], in_=den[:])
             g_p = grp.tile([P, 4 * K], BF16, tag="gp", name="g_p", align_bytes=64)
@@ -299,13 +295,17 @@ def tile_salad_pa_t_kernel(tc, f_clu, h_score, W_s2, b_s2, burst_par, out):
             st[("vt", i)] = vt
 
         def square_vt(i):
-            nc.scalar.activation(
-                out=junk_s[:], in_=st[("vt", i)][:], func=ACT.Square, accum_out=st[("x", i + 5)][:, 8:9]
-            )
+            sv = small.tile([P, 1], F32, tag="sv", name="sv")
+            nc.scalar.activation(out=junk_s[:], in_=st[("vt", i)][:], func=ACT.Square, accum_out=sv[:])
+            svm = small.tile([P, 1], F32, tag="svm", name="svm")
+            nc.gpsimd.tensor_scalar_max(out=svm[:], in0=sv[:], scalar1=1e-24)
+            rv = small.tile([P, 1], F32, tag="rv", name="rv")
+            nc.gpsimd.tensor_tensor(out=rv[:], in0=svm[:], in1=mhalf[:, 0:1], op=ALU.pow)
+            st[("rv", i)] = rv
 
         def spread_rv(i):
             rvp = paux.tile([P, K], F32, tag="aux", name="rvp")
-            nc.tensor.transpose(rvp[:], st[("y", i + 5)][:, 8:9].to_broadcast([P, P]), ident[:])
+            nc.tensor.transpose(rvp[:], st[("rv", i)][:, 0:1].to_broadcast([P, P]), ident[:])
             st[("rvp", i)] = rvp
 
         def v_rows(i):
@@ -346,41 +346,35 @@ def tile_salad_pa_t_kernel(tc, f_clu, h_score, W_s2, b_s2, burst_par, out):
 
         load(0)
         with tc.manual_schedule():
-            for r in range(-1, IMAGES + 7):
+            for r in range(-1, IMAGES + 5):
                 on(load, r + 2)
-                if 0 <= r < IMAGES + 5:
-                    st[("x", r)] = small.tile([P, 9], F32, tag="x", name="x")
                 on(scores, r - 1)
                 on(copy_out, r)
-                on(square_vt, r - 5)
-                on(fn_mult, r - 2)
-                on(tanh, r - 3, 0)
-                on(square, r, 0)
-                on(sim, r - 3, 2)
-                on(tanh, r - 3, 1)
-                on(square, r, 1)
-                on(sim, r - 3, 3)
-                on(transposes, r + 1)
                 on(h_regroup, r)
-                on(quant_ft, r)
-                on(quant_h, r)
-                on(tanh, r - 3, 2)
-                on(square, r, 2)
-                on(tanh, r - 3, 3)
-                on(square, r, 3)
-                on(spread_rn, r - 1)
-                on(spread_rv, r - 6)
-                on(v_rows, r - 6)
-                on(pmat, r - 4)
-                on(quant_fn, r - 2)
-                on(quant_p, r - 4)
-                on(exps, r - 2)
-                on(copy_rv, r - 6)
-                if 0 <= r < IMAGES + 5:
-                    powers(r)
-                on(v_transposed, r - 4)
                 on(sim, r - 2, 0)
                 on(sim, r - 2, 1)
+                on(pmat, r - 3)
+                on(squares, r)
+                on(quant_h, r)
+                on(quant_p, r - 3)
+                on(spread_rn, r - 1)
+                on(transposes, r + 1)
+                on(spread_rv, r - 4)
+                on(v_rows, r - 4)
                 on(bias_add, r - 1)
+                on(quant_ft, r)
                 on(row_max, r - 1)
-                on(final, r - 6)
+                on(tanh, r - 2, 0)
+                on(tanh, r - 2, 1)
+                on(copy_rv, r - 4)
+                on(sim, r - 2, 2)
+                on(sim, r - 2, 3)
+                on(v_transposed, r - 3)
+                on(exps, r - 2)
+                on(fn_mult, r - 1)
+                on(tanh, r - 2, 2)
+                on(tanh, r - 2, 3)
+                on(burst, r - 2)
+                on(square_vt, r - 3)
+                on(final, r - 4)
+                on(quant_fn, r - 1)

@@ -30,7 +30,7 @@ def tile_salad_pa_t_kernel(tc, f_clu, h_score, W_s2, b_s2, burst_par, out):
         qs = ctx.enter_context(tc.tile_pool(name="qs", bufs=3))
         work = ctx.enter_context(tc.tile_pool(name="work", bufs=3))
         small = ctx.enter_context(tc.tile_pool(name="small", bufs=4))
-        junkp = ctx.enter_context(tc.tile_pool(name="junkp", bufs=1))
+        junkp = ctx.enter_context(tc.tile_pool(name="junkp", bufs=6))
         pft = ctx.enter_context(tc.psum_pool(name="pft", bufs=2))
         prn = ctx.enter_context(tc.psum_pool(name="prn", bufs=1))
         psc = ctx.enter_context(tc.psum_pool(name="psc", bufs=1))
@@ -71,7 +71,8 @@ def tile_salad_pa_t_kernel(tc, f_clu, h_score, W_s2, b_s2, burst_par, out):
         w_s = const.tile([P, K], U8, name="w_s", align_bytes=64)
         nc.vector.quantize_mx(out=w_q[:].bitcast(FP8X4), scales=w_s[:], in_=g_w[:])
 
-        junk_s = junkp.tile([P, 512], BF16, name="junk_s")
+        def junk():
+            return junkp.tile([P, 512], BF16, tag="junk", name="junk_s")
 
         st = {}
 
@@ -117,7 +118,7 @@ def tile_salad_pa_t_kernel(tc, f_clu, h_score, W_s2, b_s2, burst_par, out):
             g_tv = st[("gt", i)][:].rearrange("q (c t) -> q c t", t=4)
             for t in range(4):
                 nc.scalar.activation(
-                    out=junk_s[:], in_=g_tv[:, :, t], func=ACT.Square, accum_out=ss[:, t : t + 1]
+                    out=junk()[:], in_=g_tv[:, :, t], func=ACT.Square, accum_out=ss[:, t : t + 1]
                 )
             ssm = small.tile([P, 4], F32, tag="ssm", name="ssm")
             nc.gpsimd.tensor_scalar_max(out=ssm[:], in0=ss[:], scalar1=1e-24)
@@ -239,7 +240,7 @@ def tile_salad_pa_t_kernel(tc, f_clu, h_score, W_s2, b_s2, burst_par, out):
 
         def tanh(i, t):
             nc.scalar.activation(
-                out=junk_s[:],
+                out=junk()[:],
                 in_=st[("sm", i, t)][:],
                 func=ACT.Tanh,
                 bias=half[:, 1:2],
@@ -258,12 +259,19 @@ def tile_salad_pa_t_kernel(tc, f_clu, h_score, W_s2, b_s2, burst_par, out):
             nc.gpsimd.tensor_scalar_add(out=wpe[:], in0=wp[:], scalar1=1e-6)
             st[("wpe", i)] = wpe
 
-        def pmat(i):
-            e, se = st[("e", i)]
+        def denom(i):
             den = small.tile([P, 4], F32, tag="den", name="den")
-            nc.vector.tensor_tensor(out=den[:], in0=st[("wpe", i)][:], in1=se[:], op=ALU.mult)
+            nc.vector.tensor_tensor(out=den[:], in0=st[("wpe", i)][:], in1=st[("e", i)][1][:], op=ALU.mult)
+            st[("den", i)] = den
+
+        def recip(i):
             c = small.tile([P, 4], F32, tag="c", name="c")
-            nc.vector.reciprocal(out=c[:], in_=den[:])
+            nc.vector.reciprocal(out=c[:], in_=st[("den", i)][:])
+            st[("c", i)] = c
+
+        def pmat(i):
+            e = st[("e", i)][0]
+            c = st[("c", i)]
             g_p = grp.tile([P, 4 * K], BF16, tag="gp", name="g_p", align_bytes=64)
             nc.vector.tensor_tensor(
                 out=g_p[:].rearrange("q (k t) -> q k t", t=4),
@@ -296,7 +304,7 @@ def tile_salad_pa_t_kernel(tc, f_clu, h_score, W_s2, b_s2, burst_par, out):
 
         def square_vt(i):
             sv = small.tile([P, 1], F32, tag="sv", name="sv")
-            nc.scalar.activation(out=junk_s[:], in_=st[("vt", i)][:], func=ACT.Square, accum_out=sv[:])
+            nc.scalar.activation(out=junk()[:], in_=st[("vt", i)][:], func=ACT.Square, accum_out=sv[:])
             svm = small.tile([P, 1], F32, tag="svm", name="svm")
             nc.gpsimd.tensor_scalar_max(out=svm[:], in0=sv[:], scalar1=1e-24)
             rv = small.tile([P, 1], F32, tag="rv", name="rv")
@@ -353,16 +361,18 @@ def tile_salad_pa_t_kernel(tc, f_clu, h_score, W_s2, b_s2, burst_par, out):
                 on(h_regroup, r)
                 on(sim, r - 2, 0)
                 on(sim, r - 2, 1)
-                on(pmat, r - 3)
+                on(denom, r - 3)
                 on(squares, r)
                 on(quant_h, r)
-                on(quant_p, r - 3)
+                on(recip, r - 3)
                 on(spread_rn, r - 1)
                 on(transposes, r + 1)
                 on(spread_rv, r - 4)
                 on(v_rows, r - 4)
                 on(bias_add, r - 1)
+                on(pmat, r - 3)
                 on(quant_ft, r)
+                on(quant_p, r - 3)
                 on(row_max, r - 1)
                 on(tanh, r - 2, 0)
                 on(tanh, r - 2, 1)

@@ -40,36 +40,42 @@ def tile_salad_pa_t_kernel(tc, f_clu, h_score, W_s2, b_s2, burst_par, out):
 
         ident = const.tile([P, P], F32, name="ident")
         make_identity(nc, ident[:])
-        par_bf = const.tile([P, 3], BF16, name="par_bf")
-        nc.sync.dma_start(out=par_bf[:], in_=burst_par.partition_broadcast(P))
         w_sb = const.tile([P, 512], BF16, name="w_sb")
-        nc.sync.dma_start(out=w_sb[:], in_=W_s2)
-        bias_bf = const.tile([P, K], BF16, name="bias_bf")
-        nc.sync.dma_start(out=bias_bf[:], in_=b_s2.partition_broadcast(P))
-
-        par = const.tile([P, 3], F32, name="par")
-        nc.vector.tensor_copy(out=par[:], in_=par_bf[:])
-        half = const.tile([P, 2], F32, name="half")
-        nc.vector.tensor_scalar_mul(out=half[:], in0=par[:, 0:2], scalar1=0.5)
-        pexp = const.tile([P, 4], F32, name="pexp")
-        nc.vector.tensor_copy(out=pexp[:], in_=par[:, 2:3].to_broadcast([P, 4]))
+        row0 = const.tile([P, 2 * K], BF16, name="row0")
+        nc.vector.memset(row0[:], 0.0)
+        ones = const.tile([P, P], BF16, name="ones")
+        nc.vector.memset(ones[:], 1.0)
         mhalf = const.tile([P, 4], F32, name="mhalf")
         nc.vector.memset(mhalf[:], -0.5)
-        biasb = const.tile([P, K], F32, name="biasb")
-        nc.vector.tensor_copy(out=biasb[:], in_=bias_bf[:])
-
-        wps = paux.tile([P, 2, P], F32, tag="aux", name="wps")
-        w32 = w_sb[:].bitcast(F32).rearrange("k (p u) -> k p u", u=2)
-        for u in range(2):
-            nc.tensor.transpose(wps[:, u, :], w32[:, :, u], ident[:])
+        spread = const.tile([P, 2 * K], F32, name="spread")
+        biasb = spread[:, 0:K]
+        par = spread[:, K : K + 3]
+        half = const.tile([P, 2], F32, name="half")
+        pexp = const.tile([P, 4], F32, name="pexp")
         g_w = const.tile([P, 4 * K], BF16, name="g_w", align_bytes=64)
-        nc.vector.tensor_copy(
-            out=g_w[:].bitcast(F32).rearrange("p (k u) -> p k u", u=2),
-            in_=wps[:].rearrange("p u k -> p k u"),
-        )
         w_q = const.tile([P, K], U32, name="w_q", align_bytes=64)
         w_s = const.tile([P, K], U8, name="w_s", align_bytes=64)
-        nc.vector.quantize_mx(out=w_q[:].bitcast(FP8X4), scales=w_s[:], in_=g_w[:])
+
+        def small_loads():
+            nc.sync.dma_start(out=w_sb[:], in_=W_s2)
+            nc.sync.dma_start(out=row0[0:1, 0:K], in_=b_s2.unsqueeze(0))
+            nc.sync.dma_start(out=row0[0:1, K : K + 3], in_=burst_par.unsqueeze(0))
+
+        def constants():
+            sps = paux.tile([P, 2 * K], F32, tag="aux", name="sps")
+            nc.tensor.matmul(out=sps[:], lhsT=ones[:], rhs=row0[:], start=True, stop=True)
+            nc.vector.tensor_copy(out=spread[:], in_=sps[:])
+            nc.vector.tensor_scalar_mul(out=half[:], in0=par[:, 0:2], scalar1=0.5)
+            nc.vector.tensor_copy(out=pexp[:], in_=par[:, 2:3].to_broadcast([P, 4]))
+            wps = paux.tile([P, 2, P], F32, tag="aux", name="wps")
+            w32 = w_sb[:].bitcast(F32).rearrange("k (p u) -> k p u", u=2)
+            for u in range(2):
+                nc.tensor.transpose(wps[:, u, :], w32[:, :, u], ident[:])
+            nc.vector.tensor_copy(
+                out=g_w[:].bitcast(F32).rearrange("p (k u) -> p k u", u=2),
+                in_=wps[:].rearrange("p u k -> p k u"),
+            )
+            nc.vector.quantize_mx(out=w_q[:].bitcast(FP8X4), scales=w_s[:], in_=g_w[:])
 
         def junk():
             return junkp.tile([P, 512], BF16, tag="junk", name="junk_s")
@@ -190,7 +196,7 @@ def tile_salad_pa_t_kernel(tc, f_clu, h_score, W_s2, b_s2, burst_par, out):
             nc.vector.tensor_tensor(
                 out=sb[:].rearrange("q (t k) -> q t k", t=4),
                 in0=st[("sc", i)][:].rearrange("q (t k) -> q t k", t=4),
-                in1=biasb[:].unsqueeze(1).to_broadcast([P, 4, K]),
+                in1=biasb.unsqueeze(1).to_broadcast([P, 4, K]),
                 op=ALU.add,
             )
             st[("sb", i)] = sb
@@ -352,8 +358,9 @@ def tile_salad_pa_t_kernel(tc, f_clu, h_score, W_s2, b_s2, burst_par, out):
             if 0 <= i < IMAGES:
                 step(i, *args)
 
-        load(0)
         with tc.manual_schedule():
+            load(0)
+            small_loads()
             for r in range(-1, IMAGES + 5):
                 on(load, r + 2)
                 on(scores, r - 1)
@@ -363,13 +370,13 @@ def tile_salad_pa_t_kernel(tc, f_clu, h_score, W_s2, b_s2, burst_par, out):
                 on(sim, r - 2, 1)
                 on(denom, r - 3)
                 on(squares, r)
-                on(quant_h, r)
+                on(bias_add, r - 1)
                 on(recip, r - 3)
+                on(quant_h, r)
                 on(spread_rn, r - 1)
                 on(transposes, r + 1)
                 on(spread_rv, r - 4)
                 on(v_rows, r - 4)
-                on(bias_add, r - 1)
                 on(pmat, r - 3)
                 on(quant_ft, r)
                 on(quant_p, r - 3)
@@ -388,3 +395,5 @@ def tile_salad_pa_t_kernel(tc, f_clu, h_score, W_s2, b_s2, burst_par, out):
                 on(square_vt, r - 3)
                 on(final, r - 4)
                 on(quant_fn, r - 1)
+                if r == 0:
+                    constants()

@@ -91,14 +91,14 @@ def tile_salad_pa_t_kernel(tc, f_clu, h_score, W_s2, b_s2, burst_par, out):
             st[("h", i)] = h_sb
 
         def transposes(i):
-            f32v = st[("f", i)][:].bitcast(F32).rearrange("p (j q u) -> p j q u", j=4, u=2)
+            f32v = st[("f", i)][:].bitcast(F32).rearrange("p (j u q) -> p j u q", j=4, u=2)
             banks = []
             for b in range(2):
                 ftb = pft.tile([P, 2, 256], F32, tag="ft", name="ftb")
                 for u in range(2):
                     for jj in range(2):
                         nc.tensor.transpose(
-                            ftb[:, u, jj * P : (jj + 1) * P], f32v[:, 2 * b + jj, :, u], ident[:]
+                            ftb[:, u, jj * P : (jj + 1) * P], f32v[:, 2 * b + jj, u, :], ident[:]
                         )
                 banks.append(ftb)
             st[("ftb", i)] = banks
@@ -143,15 +143,16 @@ def tile_salad_pa_t_kernel(tc, f_clu, h_score, W_s2, b_s2, burst_par, out):
 
         def fn_mult(i):
             g_f = grp.tile([P, 4 * N], BF16, tag="gf", name="g_f", align_bytes=64)
-            nc.vector.tensor_tensor(
-                out=g_f[:].rearrange("p (t q j) -> p q j t", t=4, j=4),
-                in0=st[("f", i)][:].rearrange("p (j q t) -> p q j t", j=4, t=4),
-                in1=st[("rnb", i)][:]
-                .rearrange("p (t q) -> p q t", t=4)
-                .unsqueeze(2)
-                .to_broadcast([P, P, 4, 4]),
-                op=ALU.mult,
-            )
+            g_fv = g_f[:].rearrange("p (u e q j) -> p u q j e", u=2, e=2, j=4)
+            f_v = st[("f", i)][:].rearrange("p (j u q e) -> p u q j e", j=4, u=2, e=2)
+            rn_v = st[("rnb", i)][:].rearrange("p (u e q) -> p u q e", u=2, e=2)
+            for u in range(2):
+                nc.vector.tensor_tensor(
+                    out=g_fv[:, u],
+                    in0=f_v[:, u],
+                    in1=rn_v[:, u].unsqueeze(2).to_broadcast([P, P, 4, 2]),
+                    op=ALU.mult,
+                )
             st[("gf", i)] = g_f
 
         def quant_fn(i):
@@ -163,10 +164,10 @@ def tile_salad_pa_t_kernel(tc, f_clu, h_score, W_s2, b_s2, burst_par, out):
 
         def h_regroup(i):
             g_h = grp.tile([P, 4 * N], BF16, tag="gh", name="g_h", align_bytes=64)
-            nc.vector.tensor_copy(
-                out=g_h[:].rearrange("p (t q j) -> p q j t", t=4, j=4),
-                in_=st[("h", i)][:].rearrange("p (j q t) -> p q j t", j=4, t=4),
-            )
+            g_hv = g_h[:].rearrange("p (u e q j) -> p u q j e", u=2, e=2, j=4)
+            h_v = st[("h", i)][:].rearrange("p (j u q e) -> p u q j e", j=4, u=2, e=2)
+            for u in range(2):
+                nc.vector.tensor_copy(out=g_hv[:, u], in_=h_v[:, u])
             st[("gh", i)] = g_h
 
         def quant_h(i):

@@ -35,8 +35,7 @@ def tile_salad_pa_t_kernel(tc, f_clu, h_score, W_s2, b_s2, burst_par, out):
         prn = ctx.enter_context(tc.psum_pool(name="prn", bufs=1))
         psc = ctx.enter_context(tc.psum_pool(name="psc", bufs=1))
         psim = ctx.enter_context(tc.psum_pool(name="psim", bufs=2))
-        pv = ctx.enter_context(tc.psum_pool(name="pv", bufs=1))
-        paux = ctx.enter_context(tc.psum_pool(name="paux", bufs=1))
+        paux = ctx.enter_context(tc.psum_pool(name="paux", bufs=2))
 
         ident = const.tile([P, P], F32, name="ident")
         make_identity(nc, ident[:])
@@ -47,9 +46,7 @@ def tile_salad_pa_t_kernel(tc, f_clu, h_score, W_s2, b_s2, burst_par, out):
         nc.vector.memset(ones[:], 1.0)
         mhalf = const.tile([P, 4], F32, name="mhalf")
         nc.vector.memset(mhalf[:], -0.5)
-        spread = const.tile([P, 2 * K], F32, name="spread")
-        biasb = spread[:, 0:K]
-        par = spread[:, K : K + 3]
+        bias = const.tile([P, 1], F32, name="bias")
         half = const.tile([P, 2], F32, name="half")
         pexp = const.tile([P, 4], F32, name="pexp")
         g_w = const.tile([P, 4 * K], BF16, name="g_w", align_bytes=64)
@@ -62,11 +59,12 @@ def tile_salad_pa_t_kernel(tc, f_clu, h_score, W_s2, b_s2, burst_par, out):
             nc.sync.dma_start(out=row0[0:1, K : K + 3], in_=burst_par.unsqueeze(0))
 
         def constants():
-            sps = paux.tile([P, 2 * K], F32, tag="aux", name="sps")
-            nc.tensor.matmul(out=sps[:], lhsT=ones[:], rhs=row0[:], start=True, stop=True)
-            nc.vector.tensor_copy(out=spread[:], in_=sps[:])
-            nc.vector.tensor_scalar_mul(out=half[:], in0=par[:, 0:2], scalar1=0.5)
-            nc.vector.tensor_copy(out=pexp[:], in_=par[:, 2:3].to_broadcast([P, 4]))
+            sps = paux.tile([P, 8], F32, tag="aux", name="sps")
+            nc.tensor.matmul(out=sps[:, 0:4], lhsT=row0[:, 0:K], rhs=ones[:, 0:4], start=True, stop=True)
+            nc.tensor.matmul(out=sps[:, 4:8], lhsT=ones[:], rhs=row0[:, K : K + 4], start=True, stop=True)
+            nc.vector.tensor_copy(out=bias[:], in_=sps[:, 0:1])
+            nc.vector.tensor_scalar_mul(out=half[:], in0=sps[:, 4:6], scalar1=0.5)
+            nc.vector.tensor_copy(out=pexp[:], in_=sps[:, 6:7].to_broadcast([P, 4]))
             wps = paux.tile([P, 2, P], F32, tag="aux", name="wps")
             w32 = w_sb[:].bitcast(F32).rearrange("k (p u) -> k p u", u=2)
             for u in range(2):
@@ -119,15 +117,17 @@ def tile_salad_pa_t_kernel(tc, f_clu, h_score, W_s2, b_s2, burst_par, out):
             nc.vector.quantize_mx(out=ft_q[:].bitcast(FP8X4), scales=ft_s[:], in_=st[("gt", i)][:])
             st[("ftq", i)] = (ft_q, ft_s)
 
-        def squares(i):
-            ss = small.tile([P, 4], F32, tag="ss", name="ss")
+        def squares(i, t):
+            if t == 0:
+                st[("ss", i)] = small.tile([P, 4], F32, tag="ss", name="ss")
             g_tv = st[("gt", i)][:].rearrange("q (c t) -> q c t", t=4)
-            for t in range(4):
-                nc.scalar.activation(
-                    out=junk()[:], in_=g_tv[:, :, t], func=ACT.Square, accum_out=ss[:, t : t + 1]
-                )
+            nc.scalar.activation(
+                out=junk()[:], in_=g_tv[:, :, t], func=ACT.Square, accum_out=st[("ss", i)][:, t : t + 1]
+            )
+
+        def norms(i):
             ssm = small.tile([P, 4], F32, tag="ssm", name="ssm")
-            nc.gpsimd.tensor_scalar_max(out=ssm[:], in0=ss[:], scalar1=1e-24)
+            nc.gpsimd.tensor_scalar_max(out=ssm[:], in0=st[("ss", i)][:], scalar1=1e-24)
             rn = small.tile([P, 4], F32, tag="rn", name="rn")
             nc.gpsimd.tensor_tensor(out=rn[:], in0=ssm[:], in1=mhalf[:], op=ALU.pow)
             st[("rn", i)] = rn
@@ -135,24 +135,26 @@ def tile_salad_pa_t_kernel(tc, f_clu, h_score, W_s2, b_s2, burst_par, out):
         def spread_rn(i):
             rn = st[("rn", i)]
             rnb = prn.tile([P, N], F32, tag="rnb", name="rnb")
-            for t in range(4):
-                nc.tensor.transpose(
-                    rnb[:, t * P : (t + 1) * P], rn[:, t : t + 1].to_broadcast([P, P]), ident[:]
-                )
+            for u in range(2):
+                for e in range(2):
+                    block = slice((2 * e + u) * P, (2 * e + u + 1) * P)
+                    t = 2 * u + e
+                    nc.tensor.transpose(
+                        rnb[:, block], rn[:, t : t + 1].to_broadcast([P, P]), ident[:]
+                    )
             st[("rnb", i)] = rnb
 
         def fn_mult(i):
             g_f = grp.tile([P, 4 * N], BF16, tag="gf", name="g_f", align_bytes=64)
-            g_fv = g_f[:].rearrange("p (u e q j) -> p u q j e", u=2, e=2, j=4)
-            f_v = st[("f", i)][:].rearrange("p (j u q e) -> p u q j e", j=4, u=2, e=2)
-            rn_v = st[("rnb", i)][:].rearrange("p (u e q) -> p u q e", u=2, e=2)
-            for u in range(2):
-                nc.vector.tensor_tensor(
-                    out=g_fv[:, u],
-                    in0=f_v[:, u],
-                    in1=rn_v[:, u].unsqueeze(2).to_broadcast([P, P, 4, 2]),
-                    op=ALU.mult,
-                )
+            nc.vector.tensor_tensor(
+                out=g_f[:].rearrange("p (e w j) -> p w j e", e=2, j=4),
+                in0=st[("f", i)][:].rearrange("p (j w e) -> p w j e", j=4, e=2),
+                in1=st[("rnb", i)][:]
+                .rearrange("p (e w) -> p w e", e=2)
+                .unsqueeze(2)
+                .to_broadcast([P, 2 * P, 4, 2]),
+                op=ALU.mult,
+            )
             st[("gf", i)] = g_f
 
         def quant_fn(i):
@@ -164,10 +166,10 @@ def tile_salad_pa_t_kernel(tc, f_clu, h_score, W_s2, b_s2, burst_par, out):
 
         def h_regroup(i):
             g_h = grp.tile([P, 4 * N], BF16, tag="gh", name="g_h", align_bytes=64)
-            g_hv = g_h[:].rearrange("p (u e q j) -> p u q j e", u=2, e=2, j=4)
-            h_v = st[("h", i)][:].rearrange("p (j u q e) -> p u q j e", j=4, u=2, e=2)
-            for u in range(2):
-                nc.vector.tensor_copy(out=g_hv[:, u], in_=h_v[:, u])
+            nc.vector.tensor_copy(
+                out=g_h[:].rearrange("p (c i j) -> p c j i", i=4, j=4),
+                in_=st[("h", i)][:].rearrange("p (j c i) -> p c j i", j=4, i=4),
+            )
             st[("gh", i)] = g_h
 
         def quant_h(i):
@@ -178,35 +180,42 @@ def tile_salad_pa_t_kernel(tc, f_clu, h_score, W_s2, b_s2, burst_par, out):
 
         def scores(i):
             h_q, h_s = st[("hq", i)]
-            sc = psc.tile([P, 4 * K], F32, tag="sc", name="sc")
-            for t in range(4):
-                cols = slice(t * P, (t + 1) * P)
-                nc.tensor.matmul_mx(
-                    out=sc[:, cols],
-                    lhsT=h_q[:, cols].bitcast(FP8X4),
-                    lhsT_scale=h_s[:, cols],
-                    rhs=w_q[:].bitcast(FP8X4),
-                    rhs_scale=w_s[:],
-                    start=True,
-                    stop=True,
-                )
+            sc = paux.tile([P, N], F32, tag="aux", name="sc")
+            nc.tensor.matmul_mx(
+                out=sc[:],
+                lhsT=w_q[:].bitcast(FP8X4),
+                lhsT_scale=w_s[:],
+                rhs=h_q[:].bitcast(FP8X4),
+                rhs_scale=h_s[:],
+                start=True,
+                stop=True,
+            )
             st[("sc", i)] = sc
 
         def bias_add(i):
-            sb = work.tile([P, 4 * K], F32, tag="sb", name="sb")
-            nc.vector.tensor_tensor(
-                out=sb[:].rearrange("q (t k) -> q t k", t=4),
-                in0=st[("sc", i)][:].rearrange("q (t k) -> q t k", t=4),
-                in1=biasb.unsqueeze(1).to_broadcast([P, 4, K]),
-                op=ALU.add,
+            sb = work.tile([P, N], F32, tag="sb", name="sb")
+            nc.scalar.activation(
+                out=sb[:].rearrange("k (e w) -> k e w", e=2),
+                in_=st[("sc", i)][:].rearrange("k (w e) -> k e w", e=2),
+                func=ACT.Identity,
+                bias=bias[:],
+                scale=1.0,
             )
             st[("sb", i)] = sb
+
+        def turn_scores(i):
+            sq = psc.tile([P, 4 * K], F32, tag="sq", name="sq")
+            for t in range(4):
+                nc.tensor.transpose(
+                    sq[:, t * K : (t + 1) * K], st[("sb", i)][:, t * P : (t + 1) * P], ident[:]
+                )
+            st[("sq", i)] = sq
 
         def row_max(i):
             nm = small.tile([P, 4], F32, tag="nm", name="nm")
             nc.vector.tensor_reduce(
                 out=nm[:],
-                in_=st[("sb", i)][:].rearrange("q (t k) -> q t k", t=4),
+                in_=st[("sq", i)][:].rearrange("q (t k) -> q t k", t=4),
                 axis=AX.X,
                 op=ALU.max,
                 negate=True,
@@ -214,7 +223,7 @@ def tile_salad_pa_t_kernel(tc, f_clu, h_score, W_s2, b_s2, burst_par, out):
             st[("nm", i)] = nm
 
         def exps(i):
-            sb = st[("sb", i)]
+            sq = st[("sq", i)]
             nm = st[("nm", i)]
             e = work.tile([P, 4 * K], F32, tag="e", name="e")
             se = small.tile([P, 4], F32, tag="se", name="se")
@@ -222,7 +231,7 @@ def tile_salad_pa_t_kernel(tc, f_clu, h_score, W_s2, b_s2, burst_par, out):
                 cols = slice(t * K, (t + 1) * K)
                 nc.scalar.activation(
                     out=e[:, cols],
-                    in_=sb[:, cols],
+                    in_=sq[:, cols],
                     func=ACT.Exp,
                     bias=nm[:, t : t + 1],
                     scale=1.0,
@@ -257,18 +266,23 @@ def tile_salad_pa_t_kernel(tc, f_clu, h_score, W_s2, b_s2, burst_par, out):
 
         def burst(i):
             w = small.tile([P, 4], F32, tag="w", name="w")
-            nc.gpsimd.tensor_scalar(
-                out=w[:], in0=st[("ta", i)][:], scalar1=0.5, scalar2=0.5 * N, op0=ALU.mult, op1=ALU.add
+            nc.scalar.activation(
+                out=w[:], in_=st[("ta", i)][:], func=ACT.Copy, bias=0.5 * N, scale=0.5
             )
             wp = small.tile([P, 4], F32, tag="wp", name="wp")
             nc.gpsimd.tensor_tensor(out=wp[:], in0=w[:], in1=pexp[:], op=ALU.pow)
-            wpe = small.tile([P, 4], F32, tag="wpe", name="wpe")
-            nc.gpsimd.tensor_scalar_add(out=wpe[:], in0=wp[:], scalar1=1e-6)
-            st[("wpe", i)] = wpe
+            st[("wp", i)] = wp
 
         def denom(i):
             den = small.tile([P, 4], F32, tag="den", name="den")
-            nc.vector.tensor_tensor(out=den[:], in0=st[("wpe", i)][:], in1=st[("e", i)][1][:], op=ALU.mult)
+            nc.vector.scalar_tensor_tensor(
+                out=den[:],
+                in0=st[("wp", i)][:],
+                scalar=1e-6,
+                in1=st[("e", i)][1][:],
+                op0=ALU.add,
+                op1=ALU.mult,
+            )
             st[("den", i)] = den
 
         def recip(i):
@@ -281,9 +295,9 @@ def tile_salad_pa_t_kernel(tc, f_clu, h_score, W_s2, b_s2, burst_par, out):
             c = st[("c", i)]
             g_p = grp.tile([P, 4 * K], BF16, tag="gp", name="g_p", align_bytes=64)
             nc.vector.tensor_tensor(
-                out=g_p[:].rearrange("q (k t) -> q k t", t=4),
-                in0=e[:].rearrange("q (t k) -> q k t", t=4),
-                in1=c[:].unsqueeze(1).to_broadcast([P, K, 4]),
+                out=g_p[:].rearrange("q (k u e) -> q k u e", u=2, e=2),
+                in0=e[:].rearrange("q (e u k) -> q k u e", u=2, e=2),
+                in1=c[:].rearrange("q (e u) -> q u e", e=2).unsqueeze(1).to_broadcast([P, K, 2, 2]),
                 op=ALU.mult,
             )
             st[("gp", i)] = g_p
@@ -312,10 +326,8 @@ def tile_salad_pa_t_kernel(tc, f_clu, h_score, W_s2, b_s2, burst_par, out):
         def square_vt(i):
             sv = small.tile([P, 1], F32, tag="sv", name="sv")
             nc.scalar.activation(out=junk()[:], in_=st[("vt", i)][:], func=ACT.Square, accum_out=sv[:])
-            svm = small.tile([P, 1], F32, tag="svm", name="svm")
-            nc.gpsimd.tensor_scalar_max(out=svm[:], in0=sv[:], scalar1=1e-24)
             rv = small.tile([P, 1], F32, tag="rv", name="rv")
-            nc.gpsimd.tensor_tensor(out=rv[:], in0=svm[:], in1=mhalf[:, 0:1], op=ALU.pow)
+            nc.gpsimd.tensor_tensor(out=rv[:], in0=sv[:], in1=mhalf[:, 0:1], op=ALU.pow)
             st[("rv", i)] = rv
 
         def spread_rv(i):
@@ -326,7 +338,7 @@ def tile_salad_pa_t_kernel(tc, f_clu, h_score, W_s2, b_s2, burst_par, out):
         def v_rows(i):
             ft_q, ft_s = st[("ftq", i)]
             p_q, p_s = st[("pq", i)]
-            v = pv.tile([P, 4 * K], F32, tag="v", name="v")
+            v = paux.tile([P, 4 * K], F32, tag="aux", name="v")
             for j in range(4):
                 cols = slice(j * P, (j + 1) * P)
                 nc.tensor.matmul_mx(
@@ -347,11 +359,13 @@ def tile_salad_pa_t_kernel(tc, f_clu, h_score, W_s2, b_s2, burst_par, out):
 
         def final(i):
             o = work.tile([P, 4 * K], F32, tag="o", name="o")
-            nc.vector.tensor_tensor(
+            nc.vector.scalar_tensor_tensor(
                 out=o[:].rearrange("p (j k) -> p j k", j=4),
-                in0=st[("v", i)][:].rearrange("p (j k) -> p j k", j=4),
-                in1=st[("rvs", i)][:].unsqueeze(1).to_broadcast([P, 4, K]),
-                op=ALU.mult,
+                in0=st[("rvs", i)][:].unsqueeze(1).to_broadcast([P, 4, K]),
+                scalar=1e12,
+                in1=st[("v", i)][:].rearrange("p (j k) -> p j k", j=4),
+                op0=ALU.min,
+                op1=ALU.mult,
             )
             nc.sync.dma_start(out=out[i].rearrange("(p j) k -> p (j k)", j=4), in_=o[:])
 
@@ -365,35 +379,40 @@ def tile_salad_pa_t_kernel(tc, f_clu, h_score, W_s2, b_s2, burst_par, out):
             for r in range(-1, IMAGES + 5):
                 on(load, r + 2)
                 on(scores, r - 1)
-                on(copy_out, r)
-                on(h_regroup, r)
                 on(sim, r - 2, 0)
                 on(sim, r - 2, 1)
-                on(denom, r - 3)
-                on(squares, r)
+                on(copy_out, r)
+                on(h_regroup, r)
+                on(exps, r - 2)
+                on(transposes, r + 1)
+                on(spread_rn, r - 1)
+                on(spread_rv, r - 4)
                 on(bias_add, r - 1)
+                on(v_rows, r - 4)
+                on(denom, r - 3)
+                on(quant_ft, r)
                 on(recip, r - 3)
                 on(quant_h, r)
-                on(spread_rn, r - 1)
-                on(transposes, r + 1)
-                on(spread_rv, r - 4)
-                on(v_rows, r - 4)
+                on(turn_scores, r - 1)
                 on(pmat, r - 3)
-                on(quant_ft, r)
-                on(quant_p, r - 3)
-                on(row_max, r - 1)
                 on(tanh, r - 2, 0)
                 on(tanh, r - 2, 1)
                 on(copy_rv, r - 4)
                 on(sim, r - 2, 2)
                 on(sim, r - 2, 3)
+                on(row_max, r - 1)
+                on(quant_p, r - 3)
                 on(v_transposed, r - 3)
-                on(exps, r - 2)
+                on(squares, r, 0)
+                on(squares, r, 1)
                 on(fn_mult, r - 1)
                 on(tanh, r - 2, 2)
                 on(tanh, r - 2, 3)
                 on(burst, r - 2)
                 on(square_vt, r - 3)
+                on(squares, r, 2)
+                on(squares, r, 3)
+                on(norms, r)
                 on(final, r - 4)
                 on(quant_fn, r - 1)
                 if r == 0:

@@ -167,8 +167,8 @@ def tile_salad_pa_t_kernel(tc, f_clu, h_score, W_s2, b_s2, burst_par, out):
         def h_regroup(i):
             g_h = grp.tile([P, 4 * N], BF16, tag="gh", name="g_h", align_bytes=64)
             nc.vector.tensor_copy(
-                out=g_h[:].rearrange("p (c i j) -> p c j i", i=4, j=4),
-                in_=st[("h", i)][:].rearrange("p (j c i) -> p c j i", j=4, i=4),
+                out=g_h[:].rearrange("p (e w j) -> p w j e", e=2, j=4),
+                in_=st[("h", i)][:].rearrange("p (j w e) -> p w j e", j=4, e=2),
             )
             st[("gh", i)] = g_h
 
@@ -195,8 +195,8 @@ def tile_salad_pa_t_kernel(tc, f_clu, h_score, W_s2, b_s2, burst_par, out):
         def bias_add(i):
             sb = work.tile([P, N], F32, tag="sb", name="sb")
             nc.scalar.activation(
-                out=sb[:].rearrange("k (e w) -> k e w", e=2),
-                in_=st[("sc", i)][:].rearrange("k (w e) -> k e w", e=2),
+                out=sb[:],
+                in_=st[("sc", i)][:],
                 func=ACT.Identity,
                 bias=bias[:],
                 scale=1.0,

@@ -80,12 +80,14 @@ def tile_salad_pa_t_kernel(tc, f_clu, h_score, W_s2, b_s2, burst_par, out):
 
         st = {}
 
-        def load(i):
+        def load_f(i):
             f_sb = ld.tile([P, 4 * N], BF16, tag="f", name="f_sb", bufs=4)
             nc.sync.dma_start(out=f_sb[:], in_=f_clu[i].rearrange("(p j) n -> p (j n)", j=4))
+            st[("f", i)] = f_sb
+
+        def load_h(i):
             h_sb = ld.tile([P, 4 * N], BF16, tag="h", name="h_sb", bufs=3)
             nc.sync.dma_start(out=h_sb[:], in_=h_score[i].rearrange("(p j) n -> p (j n)", j=4))
-            st[("f", i)] = f_sb
             st[("h", i)] = h_sb
 
         def transposes(i):
@@ -374,46 +376,48 @@ def tile_salad_pa_t_kernel(tc, f_clu, h_score, W_s2, b_s2, burst_par, out):
                 step(i, *args)
 
         with tc.manual_schedule():
-            load(0)
+            load_f(0)
+            load_h(0)
             small_loads()
             for r in range(-1, IMAGES + 5):
-                on(load, r + 2)
-                on(scores, r - 1)
+                on(load_f, r + 2)
+                on(load_h, r + 1)
+                on(scores, r - 2)
+                on(copy_out, r)
+                on(h_regroup, r - 1)
+                on(transposes, r + 1)
+                on(quant_fn, r - 2)
+                on(exps, r - 3)
+                on(spread_rn, r - 1)
                 on(sim, r - 2, 0)
                 on(sim, r - 2, 1)
-                on(copy_out, r)
-                on(h_regroup, r)
-                on(exps, r - 2)
-                on(transposes, r + 1)
-                on(spread_rn, r - 1)
-                on(spread_rv, r - 4)
-                on(bias_add, r - 1)
-                on(v_rows, r - 4)
-                on(denom, r - 3)
+                on(bias_add, r - 2)
                 on(quant_ft, r)
+                on(quant_h, r - 1)
+                on(turn_scores, r - 2)
+                on(denom, r - 3)
+                on(row_max, r - 2)
                 on(recip, r - 3)
-                on(quant_h, r)
-                on(turn_scores, r - 1)
+                on(squares, r, 0)
+                on(squares, r, 1)
+                on(squares, r, 2)
+                on(squares, r, 3)
+                on(norms, r)
+                on(spread_rv, r - 4)
+                on(v_rows, r - 4)
                 on(pmat, r - 3)
+                on(quant_p, r - 3)
+                on(v_transposed, r - 3)
                 on(tanh, r - 2, 0)
                 on(tanh, r - 2, 1)
                 on(copy_rv, r - 4)
                 on(sim, r - 2, 2)
                 on(sim, r - 2, 3)
-                on(row_max, r - 1)
-                on(quant_p, r - 3)
-                on(v_transposed, r - 3)
-                on(squares, r, 0)
-                on(squares, r, 1)
-                on(fn_mult, r - 1)
                 on(tanh, r - 2, 2)
                 on(tanh, r - 2, 3)
                 on(burst, r - 2)
                 on(square_vt, r - 3)
-                on(squares, r, 2)
-                on(squares, r, 3)
-                on(norms, r)
+                on(fn_mult, r - 1)
                 on(final, r - 4)
-                on(quant_fn, r - 1)
                 if r == 0:
                     constants()

@@ -26,14 +26,14 @@ def tile_salad_pa_t_kernel(tc, f_clu, h_score, W_s2, b_s2, burst_par, out):
         const = ctx.enter_context(tc.tile_pool(name="const", bufs=1))
         ld = ctx.enter_context(tc.tile_pool(name="ld", bufs=4))
         grp = ctx.enter_context(tc.tile_pool(name="grp", bufs=2))
-        qf = ctx.enter_context(tc.tile_pool(name="qf", bufs=5))
+        qf = ctx.enter_context(tc.tile_pool(name="qf", bufs=6))
         qs = ctx.enter_context(tc.tile_pool(name="qs", bufs=3))
         work = ctx.enter_context(tc.tile_pool(name="work", bufs=3))
-        small = ctx.enter_context(tc.tile_pool(name="small", bufs=4))
+        small = ctx.enter_context(tc.tile_pool(name="small", bufs=6))
         junkp = ctx.enter_context(tc.tile_pool(name="junkp", bufs=6))
         pft = ctx.enter_context(tc.psum_pool(name="pft", bufs=2))
-        prn = ctx.enter_context(tc.psum_pool(name="prn", bufs=1))
         psc = ctx.enter_context(tc.psum_pool(name="psc", bufs=1))
+        prn = ctx.enter_context(tc.psum_pool(name="prn", bufs=1))
         psim = ctx.enter_context(tc.psum_pool(name="psim", bufs=2))
         paux = ctx.enter_context(tc.psum_pool(name="paux", bufs=2))
 
@@ -44,11 +44,10 @@ def tile_salad_pa_t_kernel(tc, f_clu, h_score, W_s2, b_s2, burst_par, out):
         nc.vector.memset(row0[:], 0.0)
         ones = const.tile([P, P], BF16, name="ones")
         nc.vector.memset(ones[:], 1.0)
-        mhalf = const.tile([P, 4], F32, name="mhalf")
-        nc.vector.memset(mhalf[:], -0.5)
-        bias = const.tile([P, 1], F32, name="bias")
+        expo = const.tile([P, 9], F32, name="expo")
+        nc.vector.memset(expo[:], -0.5)
+        bias = const.tile([P, K], F32, name="bias")
         half = const.tile([P, 2], F32, name="half")
-        pexp = const.tile([P, 4], F32, name="pexp")
         g_w = const.tile([P, 4 * K], BF16, name="g_w", align_bytes=64)
         w_q = const.tile([P, K], U32, name="w_q", align_bytes=64)
         w_s = const.tile([P, K], U8, name="w_s", align_bytes=64)
@@ -59,12 +58,13 @@ def tile_salad_pa_t_kernel(tc, f_clu, h_score, W_s2, b_s2, burst_par, out):
             nc.sync.dma_start(out=row0[0:1, K : K + 3], in_=burst_par.unsqueeze(0))
 
         def constants():
-            sps = paux.tile([P, 8], F32, tag="aux", name="sps")
-            nc.tensor.matmul(out=sps[:, 0:4], lhsT=row0[:, 0:K], rhs=ones[:, 0:4], start=True, stop=True)
-            nc.tensor.matmul(out=sps[:, 4:8], lhsT=ones[:], rhs=row0[:, K : K + 4], start=True, stop=True)
-            nc.vector.tensor_copy(out=bias[:], in_=sps[:, 0:1])
-            nc.vector.tensor_scalar_mul(out=half[:], in0=sps[:, 4:6], scalar1=0.5)
-            nc.vector.tensor_copy(out=pexp[:], in_=sps[:, 6:7].to_broadcast([P, 4]))
+            sps = paux.tile([P, K + 4], F32, tag="aux", name="sps")
+            nc.tensor.matmul(
+                out=sps[:], lhsT=ones[:], rhs=row0[:, 0 : K + 4], start=True, stop=True
+            )
+            nc.vector.tensor_copy(out=bias[:], in_=sps[:, 0:K])
+            nc.vector.tensor_scalar_mul(out=half[:], in0=sps[:, K : K + 2], scalar1=0.5)
+            nc.vector.tensor_copy(out=expo[:, 4:8], in_=sps[:, K + 2 : K + 3].to_broadcast([P, 4]))
             wps = paux.tile([P, 2, P], F32, tag="aux", name="wps")
             w32 = w_sb[:].bitcast(F32).rearrange("k (p u) -> k p u", u=2)
             for u in range(2):
@@ -81,12 +81,12 @@ def tile_salad_pa_t_kernel(tc, f_clu, h_score, W_s2, b_s2, burst_par, out):
         st = {}
 
         def load_f(i):
-            f_sb = ld.tile([P, 4 * N], BF16, tag="f", name="f_sb", bufs=4)
+            f_sb = ld.tile([P, 4 * N], BF16, tag="f", name="f_sb", bufs=5)
             nc.sync.dma_start(out=f_sb[:], in_=f_clu[i].rearrange("(p j) n -> p (j n)", j=4))
             st[("f", i)] = f_sb
 
         def load_h(i):
-            h_sb = ld.tile([P, 4 * N], BF16, tag="h", name="h_sb", bufs=3)
+            h_sb = ld.tile([P, 4 * N], BF16, tag="h", name="h_sb", bufs=4)
             nc.sync.dma_start(out=h_sb[:], in_=h_score[i].rearrange("(p j) n -> p (j n)", j=4))
             st[("h", i)] = h_sb
 
@@ -127,15 +127,26 @@ def tile_salad_pa_t_kernel(tc, f_clu, h_score, W_s2, b_s2, burst_par, out):
                 out=junk()[:], in_=g_tv[:, :, t], func=ACT.Square, accum_out=st[("ss", i)][:, t : t + 1]
             )
 
-        def norms(i):
-            ssm = small.tile([P, 4], F32, tag="ssm", name="ssm")
-            nc.gpsimd.tensor_scalar_max(out=ssm[:], in0=st[("ss", i)][:], scalar1=1e-24)
-            rn = small.tile([P, 4], F32, tag="rn", name="rn")
-            nc.gpsimd.tensor_tensor(out=rn[:], in0=ssm[:], in1=mhalf[:], op=ALU.pow)
-            st[("rn", i)] = rn
+        def bases(r):
+            if ("bases", r) not in st:
+                st[("bases", r)] = small.tile([P, 9], F32, tag="bases", name="bases")
+            return st[("bases", r)]
+
+        def guard(i):
+            nc.gpsimd.tensor_scalar_max(out=bases(i)[:, 0:4], in0=st[("ss", i)][:], scalar1=1e-24)
+
+        def powers(r, first, last):
+            if ("pw", r) not in st:
+                st[("pw", r)] = small.tile([P, 9], F32, tag="pw", name="pw")
+            nc.gpsimd.tensor_tensor(
+                out=st[("pw", r)][:, first:last],
+                in0=bases(r)[:, first:last],
+                in1=expo[:, first:last],
+                op=ALU.pow,
+            )
 
         def spread_rn(i):
-            rn = st[("rn", i)]
+            rn = st[("pw", i)]
             rnb = prn.tile([P, N], F32, tag="rnb", name="rnb")
             for u in range(2):
                 for e in range(2):
@@ -166,13 +177,23 @@ def tile_salad_pa_t_kernel(tc, f_clu, h_score, W_s2, b_s2, burst_par, out):
             st[("fnq", i)] = (fn_q, fn_s)
             st[("ta", i)] = small.tile([P, 4], F32, tag="ta", name="ta")
 
-        def h_regroup(i):
-            g_h = grp.tile([P, 4 * N], BF16, tag="gh", name="g_h", align_bytes=64)
-            nc.vector.tensor_copy(
-                out=g_h[:].rearrange("p (e w j) -> p w j e", e=2, j=4),
-                in_=st[("h", i)][:].rearrange("p (j w e) -> p w j e", j=4, e=2),
-            )
+        def h_part(i):
+            g_h = grp.tile([P, 4 * N], BF16, tag="gh", name="g_h", bufs=1, align_bytes=64)
             st[("gh", i)] = g_h
+            nc.gpsimd.tensor_scalar(
+                out=g_h[:].rearrange("p (e w j) -> p e w j", e=2, j=4)[:, 1],
+                in0=st[("h", i)][:].rearrange("p (j w e) -> p e w j", j=4, e=2)[:, 1],
+                scalar1=1.0,
+                scalar2=0.0,
+                op0=ALU.mult,
+                op1=ALU.add,
+            )
+
+        def h_regroup(i):
+            nc.vector.tensor_copy(
+                out=st[("gh", i)][:].rearrange("p (e w j) -> p e w j", e=2, j=4)[:, 0],
+                in_=st[("h", i)][:].rearrange("p (j w e) -> p e w j", j=4, e=2)[:, 0],
+            )
 
         def quant_h(i):
             h_q = qs.tile([P, N], U32, tag="hq", name="h_q", align_bytes=64)
@@ -182,42 +203,35 @@ def tile_salad_pa_t_kernel(tc, f_clu, h_score, W_s2, b_s2, burst_par, out):
 
         def scores(i):
             h_q, h_s = st[("hq", i)]
-            sc = paux.tile([P, N], F32, tag="aux", name="sc")
-            nc.tensor.matmul_mx(
-                out=sc[:],
-                lhsT=w_q[:].bitcast(FP8X4),
-                lhsT_scale=w_s[:],
-                rhs=h_q[:].bitcast(FP8X4),
-                rhs_scale=h_s[:],
-                start=True,
-                stop=True,
-            )
+            sc = psc.tile([P, 4 * K], F32, tag="sc", name="sc")
+            for t in range(4):
+                cols = slice(t * P, (t + 1) * P)
+                nc.tensor.matmul_mx(
+                    out=sc[:, t * K : (t + 1) * K],
+                    lhsT=h_q[:, cols].bitcast(FP8X4),
+                    lhsT_scale=h_s[:, cols],
+                    rhs=w_q[:].bitcast(FP8X4),
+                    rhs_scale=w_s[:],
+                    start=True,
+                    stop=True,
+                )
             st[("sc", i)] = sc
 
         def bias_add(i):
-            sb = work.tile([P, N], F32, tag="sb", name="sb")
-            nc.scalar.activation(
-                out=sb[:],
-                in_=st[("sc", i)][:],
-                func=ACT.Identity,
-                bias=bias[:],
-                scale=1.0,
+            sb = work.tile([P, 4 * K], F32, tag="sb", name="sb")
+            nc.vector.tensor_tensor(
+                out=sb[:].rearrange("q (t k) -> q t k", t=4),
+                in0=st[("sc", i)][:].rearrange("q (t k) -> q t k", t=4),
+                in1=bias[:].unsqueeze(1).to_broadcast([P, 4, K]),
+                op=ALU.add,
             )
             st[("sb", i)] = sb
-
-        def turn_scores(i):
-            sq = psc.tile([P, 4 * K], F32, tag="sq", name="sq")
-            for t in range(4):
-                nc.tensor.transpose(
-                    sq[:, t * K : (t + 1) * K], st[("sb", i)][:, t * P : (t + 1) * P], ident[:]
-                )
-            st[("sq", i)] = sq
 
         def row_max(i):
             nm = small.tile([P, 4], F32, tag="nm", name="nm")
             nc.vector.tensor_reduce(
                 out=nm[:],
-                in_=st[("sq", i)][:].rearrange("q (t k) -> q t k", t=4),
+                in_=st[("sb", i)][:].rearrange("q (t k) -> q t k", t=4),
                 axis=AX.X,
                 op=ALU.max,
                 negate=True,
@@ -225,15 +239,15 @@ def tile_salad_pa_t_kernel(tc, f_clu, h_score, W_s2, b_s2, burst_par, out):
             st[("nm", i)] = nm
 
         def exps(i):
-            sq = st[("sq", i)]
+            sb = st[("sb", i)]
             nm = st[("nm", i)]
-            e = work.tile([P, 4 * K], F32, tag="e", name="e")
+            e = work.tile([P, 4 * K], F32, tag="e", name="e", bufs=5)
             se = small.tile([P, 4], F32, tag="se", name="se")
             for t in range(4):
                 cols = slice(t * K, (t + 1) * K)
                 nc.scalar.activation(
                     out=e[:, cols],
-                    in_=sq[:, cols],
+                    in_=sb[:, cols],
                     func=ACT.Exp,
                     bias=nm[:, t : t + 1],
                     scale=1.0,
@@ -267,19 +281,19 @@ def tile_salad_pa_t_kernel(tc, f_clu, h_score, W_s2, b_s2, burst_par, out):
             )
 
         def burst(i):
-            w = small.tile([P, 4], F32, tag="w", name="w")
             nc.scalar.activation(
-                out=w[:], in_=st[("ta", i)][:], func=ACT.Copy, bias=0.5 * N, scale=0.5
+                out=bases(i + 3)[:, 4:8],
+                in_=st[("ta", i)][:],
+                func=ACT.Copy,
+                bias=0.5 * N,
+                scale=0.5,
             )
-            wp = small.tile([P, 4], F32, tag="wp", name="wp")
-            nc.gpsimd.tensor_tensor(out=wp[:], in0=w[:], in1=pexp[:], op=ALU.pow)
-            st[("wp", i)] = wp
 
         def denom(i):
             den = small.tile([P, 4], F32, tag="den", name="den")
             nc.vector.scalar_tensor_tensor(
                 out=den[:],
-                in0=st[("wp", i)][:],
+                in0=st[("pw", i + 3)][:, 4:8],
                 scalar=1e-6,
                 in1=st[("e", i)][1][:],
                 op0=ALU.add,
@@ -326,15 +340,16 @@ def tile_salad_pa_t_kernel(tc, f_clu, h_score, W_s2, b_s2, burst_par, out):
             st[("vt", i)] = vt
 
         def square_vt(i):
-            sv = small.tile([P, 1], F32, tag="sv", name="sv")
-            nc.scalar.activation(out=junk()[:], in_=st[("vt", i)][:], func=ACT.Square, accum_out=sv[:])
-            rv = small.tile([P, 1], F32, tag="rv", name="rv")
-            nc.gpsimd.tensor_tensor(out=rv[:], in0=sv[:], in1=mhalf[:, 0:1], op=ALU.pow)
-            st[("rv", i)] = rv
+            nc.scalar.activation(
+                out=junk()[:],
+                in_=st[("vt", i)][:],
+                func=ACT.Square,
+                accum_out=bases(i + 4)[:, 8:9],
+            )
 
         def spread_rv(i):
             rvp = paux.tile([P, K], F32, tag="aux", name="rvp")
-            nc.tensor.transpose(rvp[:], st[("rv", i)][:, 0:1].to_broadcast([P, P]), ident[:])
+            nc.tensor.transpose(rvp[:], st[("pw", i + 4)][:, 8:9].to_broadcast([P, P]), ident[:])
             st[("rvp", i)] = rvp
 
         def v_rows(i):
@@ -379,45 +394,51 @@ def tile_salad_pa_t_kernel(tc, f_clu, h_score, W_s2, b_s2, burst_par, out):
             load_f(0)
             load_h(0)
             small_loads()
-            for r in range(-1, IMAGES + 5):
+            for r in range(-1, IMAGES + 6):
                 on(load_f, r + 2)
-                on(load_h, r + 1)
-                on(scores, r - 2)
+                on(load_h, r + 2)
+                on(scores, r - 1)
+                on(fn_mult, r - 2)
+                on(tanh, r - 3, 0)
+                on(tanh, r - 3, 1)
+                on(sim, r - 3, 2)
+                on(sim, r - 3, 3)
+                on(tanh, r - 3, 2)
+                on(tanh, r - 3, 3)
+                on(final, r - 6)
+                on(burst, r - 3)
+                on(h_part, r)
+                on(bias_add, r - 1)
                 on(copy_out, r)
-                on(h_regroup, r - 1)
-                on(transposes, r + 1)
-                on(quant_fn, r - 2)
-                on(exps, r - 3)
+                on(row_max, r - 1)
                 on(spread_rn, r - 1)
-                on(sim, r - 2, 0)
-                on(sim, r - 2, 1)
-                on(bias_add, r - 2)
-                on(quant_ft, r)
-                on(quant_h, r - 1)
-                on(turn_scores, r - 2)
-                on(denom, r - 3)
-                on(row_max, r - 2)
-                on(recip, r - 3)
+                on(spread_rv, r - 5)
+                on(transposes, r + 1)
+                on(exps, r - 1)
+                on(v_rows, r - 5)
+                on(denom, r - 4)
+                on(quant_fn, r - 2)
+                on(recip, r - 4)
                 on(squares, r, 0)
                 on(squares, r, 1)
+                on(copy_rv, r - 5)
+                on(sim, r - 2, 0)
+                on(sim, r - 2, 1)
+                on(pmat, r - 4)
                 on(squares, r, 2)
                 on(squares, r, 3)
-                on(norms, r)
-                on(spread_rv, r - 4)
-                on(v_rows, r - 4)
-                on(pmat, r - 3)
-                on(quant_p, r - 3)
-                on(v_transposed, r - 3)
-                on(tanh, r - 2, 0)
-                on(tanh, r - 2, 1)
-                on(copy_rv, r - 4)
-                on(sim, r - 2, 2)
-                on(sim, r - 2, 3)
-                on(tanh, r - 2, 2)
-                on(tanh, r - 2, 3)
-                on(burst, r - 2)
-                on(square_vt, r - 3)
-                on(fn_mult, r - 1)
-                on(final, r - 4)
+                on(guard, r)
+                on(quant_ft, r)
+                on(quant_p, r - 4)
+                on(v_transposed, r - 4)
+                on(h_regroup, r)
+                on(square_vt, r - 4)
+                on(quant_h, r)
+                if 0 <= r < IMAGES + 4:
+                    powers(
+                        r,
+                        0 if r < IMAGES else 4 if r < IMAGES + 3 else 8,
+                        9 if r >= 4 else 8 if r >= 3 else 4,
+                    )
                 if r == 0:
                     constants()

@@ -26,10 +26,10 @@ def tile_salad_pa_t_kernel(tc, f_clu, h_score, W_s2, b_s2, burst_par, out):
         const = ctx.enter_context(tc.tile_pool(name="const", bufs=1))
         ld = ctx.enter_context(tc.tile_pool(name="ld", bufs=4))
         grp = ctx.enter_context(tc.tile_pool(name="grp", bufs=2))
-        qf = ctx.enter_context(tc.tile_pool(name="qf", bufs=6))
+        qf = ctx.enter_context(tc.tile_pool(name="qf", bufs=7))
         qs = ctx.enter_context(tc.tile_pool(name="qs", bufs=3))
         work = ctx.enter_context(tc.tile_pool(name="work", bufs=3))
-        small = ctx.enter_context(tc.tile_pool(name="small", bufs=6))
+        small = ctx.enter_context(tc.tile_pool(name="small", bufs=7))
         junkp = ctx.enter_context(tc.tile_pool(name="junkp", bufs=6))
         pft = ctx.enter_context(tc.psum_pool(name="pft", bufs=2))
         psc = ctx.enter_context(tc.psum_pool(name="psc", bufs=1))
@@ -177,23 +177,13 @@ def tile_salad_pa_t_kernel(tc, f_clu, h_score, W_s2, b_s2, burst_par, out):
             st[("fnq", i)] = (fn_q, fn_s)
             st[("ta", i)] = small.tile([P, 4], F32, tag="ta", name="ta")
 
-        def h_part(i):
-            g_h = grp.tile([P, 4 * N], BF16, tag="gh", name="g_h", bufs=1, align_bytes=64)
-            st[("gh", i)] = g_h
-            nc.gpsimd.tensor_scalar(
-                out=g_h[:].rearrange("p (e w j) -> p e w j", e=2, j=4)[:, 1],
-                in0=st[("h", i)][:].rearrange("p (j w e) -> p e w j", j=4, e=2)[:, 1],
-                scalar1=1.0,
-                scalar2=0.0,
-                op0=ALU.mult,
-                op1=ALU.add,
-            )
-
         def h_regroup(i):
+            g_h = grp.tile([P, 4 * N], BF16, tag="gh", name="g_h", align_bytes=64)
             nc.vector.tensor_copy(
-                out=st[("gh", i)][:].rearrange("p (e w j) -> p e w j", e=2, j=4)[:, 0],
-                in_=st[("h", i)][:].rearrange("p (j w e) -> p e w j", j=4, e=2)[:, 0],
+                out=g_h[:].rearrange("p (e w j) -> p w j e", e=2, j=4),
+                in_=st[("h", i)][:].rearrange("p (j w e) -> p w j e", j=4, e=2),
             )
+            st[("gh", i)] = g_h
 
         def quant_h(i):
             h_q = qs.tile([P, N], U32, tag="hq", name="h_q", align_bytes=64)
@@ -306,11 +296,11 @@ def tile_salad_pa_t_kernel(tc, f_clu, h_score, W_s2, b_s2, burst_par, out):
             nc.vector.reciprocal(out=c[:], in_=st[("den", i)][:])
             st[("c", i)] = c
 
-        def pmat(i):
+        def pmat(i, engine):
             e = st[("e", i)][0]
             c = st[("c", i)]
             g_p = grp.tile([P, 4 * K], BF16, tag="gp", name="g_p", align_bytes=64)
-            nc.vector.tensor_tensor(
+            engine.tensor_tensor(
                 out=g_p[:].rearrange("q (k u e) -> q k u e", u=2, e=2),
                 in0=e[:].rearrange("q (e u k) -> q k u e", u=2, e=2),
                 in1=c[:].rearrange("q (e u) -> q u e", e=2).unsqueeze(1).to_broadcast([P, K, 2, 2]),
@@ -344,12 +334,12 @@ def tile_salad_pa_t_kernel(tc, f_clu, h_score, W_s2, b_s2, burst_par, out):
                 out=junk()[:],
                 in_=st[("vt", i)][:],
                 func=ACT.Square,
-                accum_out=bases(i + 4)[:, 8:9],
+                accum_out=bases(i + 5)[:, 8:9],
             )
 
         def spread_rv(i):
             rvp = paux.tile([P, K], F32, tag="aux", name="rvp")
-            nc.tensor.transpose(rvp[:], st[("pw", i + 4)][:, 8:9].to_broadcast([P, P]), ident[:])
+            nc.tensor.transpose(rvp[:], st[("pw", i + 5)][:, 8:9].to_broadcast([P, P]), ident[:])
             st[("rvp", i)] = rvp
 
         def v_rows(i):
@@ -392,9 +382,9 @@ def tile_salad_pa_t_kernel(tc, f_clu, h_score, W_s2, b_s2, burst_par, out):
 
         with tc.manual_schedule():
             load_f(0)
-            load_h(0)
             small_loads()
-            for r in range(-1, IMAGES + 6):
+            load_h(0)
+            for r in range(-1, IMAGES + 7):
                 on(load_f, r + 2)
                 on(load_h, r + 2)
                 on(scores, r - 1)
@@ -405,40 +395,39 @@ def tile_salad_pa_t_kernel(tc, f_clu, h_score, W_s2, b_s2, burst_par, out):
                 on(sim, r - 3, 3)
                 on(tanh, r - 3, 2)
                 on(tanh, r - 3, 3)
-                on(final, r - 6)
-                on(burst, r - 3)
-                on(h_part, r)
                 on(bias_add, r - 1)
+                on(pmat, r - 5, nc.gpsimd)
                 on(copy_out, r)
+                on(burst, r - 3)
+                on(final, r - 7)
                 on(row_max, r - 1)
-                on(spread_rn, r - 1)
-                on(spread_rv, r - 5)
                 on(transposes, r + 1)
-                on(exps, r - 1)
-                on(v_rows, r - 5)
+                on(spread_rn, r - 1)
+                on(spread_rv, r - 6)
+                on(exps, r - 2)
                 on(denom, r - 4)
                 on(quant_fn, r - 2)
-                on(recip, r - 4)
+                on(quant_p, r - 5)
                 on(squares, r, 0)
                 on(squares, r, 1)
-                on(copy_rv, r - 5)
+                on(recip, r - 4)
+                on(v_rows, r - 6)
+                on(copy_rv, r - 6)
+                on(v_transposed, r - 5)
+                on(h_regroup, r)
                 on(sim, r - 2, 0)
                 on(sim, r - 2, 1)
-                on(pmat, r - 4)
                 on(squares, r, 2)
                 on(squares, r, 3)
                 on(guard, r)
                 on(quant_ft, r)
-                on(quant_p, r - 4)
-                on(v_transposed, r - 4)
-                on(h_regroup, r)
-                on(square_vt, r - 4)
+                on(square_vt, r - 5)
                 on(quant_h, r)
-                if 0 <= r < IMAGES + 4:
+                if 0 <= r < IMAGES + 5:
                     powers(
                         r,
                         0 if r < IMAGES else 4 if r < IMAGES + 3 else 8,
-                        9 if r >= 4 else 8 if r >= 3 else 4,
+                        9 if r >= 5 else 8 if r >= 3 else 4,
                     )
-                if r == 0:
+                if r == -1:
                     constants()

@@ -133,7 +133,7 @@ def tile_salad_pa_t_kernel(tc, f_clu, h_score, W_s2, b_s2, burst_par, out):
             return st[("bases", r)]
 
         def guard(i):
-            nc.gpsimd.tensor_scalar_max(out=bases(i)[:, 0:4], in0=st[("ss", i)][:], scalar1=1e-24)
+            nc.vector.tensor_scalar_max(out=bases(i)[:, 0:4], in0=st[("ss", i)][:], scalar1=1e-24)
 
         def powers(r, first, last):
             if ("pw", r) not in st:
@@ -309,8 +309,8 @@ def tile_salad_pa_t_kernel(tc, f_clu, h_score, W_s2, b_s2, burst_par, out):
             st[("gp", i)] = g_p
 
         def quant_p(i):
-            p_q = qs.tile([P, K], U32, tag="pq", name="p_q", align_bytes=64)
-            p_s = qs.tile([P, K], U8, tag="ps", name="p_s", align_bytes=64)
+            p_q = qs.tile([P, K], U32, tag="pq", name="p_q", bufs=6, align_bytes=64)
+            p_s = qs.tile([P, K], U8, tag="ps", name="p_s", bufs=6, align_bytes=64)
             nc.vector.quantize_mx(out=p_q[:].bitcast(FP8X4), scales=p_s[:], in_=st[("gp", i)][:])
             st[("pq", i)] = (p_q, p_s)
 
@@ -342,10 +342,10 @@ def tile_salad_pa_t_kernel(tc, f_clu, h_score, W_s2, b_s2, burst_par, out):
             nc.tensor.transpose(rvp[:], st[("pw", i + 5)][:, 8:9].to_broadcast([P, P]), ident[:])
             st[("rvp", i)] = rvp
 
-        def v_rows(i):
+        def v_rows(i, pool=paux, tag="aux"):
             ft_q, ft_s = st[("ftq", i)]
             p_q, p_s = st[("pq", i)]
-            v = paux.tile([P, 4 * K], F32, tag="aux", name="v")
+            v = pool.tile([P, 4 * K], F32, tag=tag, name="v")
             for j in range(4):
                 cols = slice(j * P, (j + 1) * P)
                 nc.tensor.matmul_mx(
@@ -384,7 +384,7 @@ def tile_salad_pa_t_kernel(tc, f_clu, h_score, W_s2, b_s2, burst_par, out):
             load_f(0)
             small_loads()
             load_h(0)
-            for r in range(-1, IMAGES + 7):
+            for r in range(-1, IMAGES + 0):
                 on(load_f, r + 2)
                 on(load_h, r + 2)
                 on(scores, r - 1)
@@ -419,15 +419,107 @@ def tile_salad_pa_t_kernel(tc, f_clu, h_score, W_s2, b_s2, burst_par, out):
                 on(sim, r - 2, 1)
                 on(squares, r, 2)
                 on(squares, r, 3)
-                on(guard, r)
                 on(quant_ft, r)
                 on(square_vt, r - 5)
                 on(quant_h, r)
-                if 0 <= r < IMAGES + 5:
-                    powers(
-                        r,
-                        0 if r < IMAGES else 4 if r < IMAGES + 3 else 8,
-                        9 if r >= 5 else 8 if r >= 3 else 4,
-                    )
+                on(guard, r)
+                if r >= 0:
+                    powers(r, 0, 9 if r >= 5 else 8 if r >= 3 else 4)
                 if r == -1:
                     constants()
+            fn_mult(IMAGES - 2)
+            scores(IMAGES - 1)
+            tanh(IMAGES - 3, 0)
+            tanh(IMAGES - 3, 1)
+            sim(IMAGES - 3, 2)
+            sim(IMAGES - 3, 3)
+            tanh(IMAGES - 3, 2)
+            tanh(IMAGES - 3, 3)
+            burst(IMAGES - 3)
+            final(IMAGES - 7)
+            exps(IMAGES - 2)
+            powers(IMAGES + 0, 4, 8)
+            spread_rn(IMAGES - 1)
+            bias_add(IMAGES - 1)
+            spread_rv(IMAGES - 6)
+            v_rows(IMAGES - 6, pft, "ft")
+            row_max(IMAGES - 1)
+            quant_fn(IMAGES - 2)
+            copy_rv(IMAGES - 6)
+            fn_mult(IMAGES - 1)
+            sim(IMAGES - 2, 0)
+            sim(IMAGES - 2, 1)
+            tanh(IMAGES - 2, 0)
+            tanh(IMAGES - 2, 1)
+            sim(IMAGES - 2, 2)
+            sim(IMAGES - 2, 3)
+            tanh(IMAGES - 2, 2)
+            pmat(IMAGES - 5, nc.vector)
+            tanh(IMAGES - 2, 3)
+            quant_fn(IMAGES - 1)
+            denom(IMAGES - 4)
+            quant_p(IMAGES - 5)
+            burst(IMAGES - 2)
+            sim(IMAGES - 1, 0)
+            recip(IMAGES - 4)
+            sim(IMAGES - 1, 1)
+            powers(IMAGES + 1, 4, 8)
+            final(IMAGES - 6)
+            tanh(IMAGES - 1, 0)
+            v_transposed(IMAGES - 5)
+            pmat(IMAGES - 4, nc.vector)
+            tanh(IMAGES - 1, 1)
+            sim(IMAGES - 1, 2)
+            sim(IMAGES - 1, 3)
+            denom(IMAGES - 3)
+            quant_p(IMAGES - 4)
+            square_vt(IMAGES - 5)
+            recip(IMAGES - 3)
+            denom(IMAGES - 2)
+            v_transposed(IMAGES - 4)
+            pmat(IMAGES - 3, nc.vector)
+            tanh(IMAGES - 1, 2)
+            tanh(IMAGES - 1, 3)
+            burst(IMAGES - 1)
+            exps(IMAGES - 1)
+            powers(IMAGES + 0, 8, 9)
+            recip(IMAGES - 2)
+            quant_p(IMAGES - 3)
+            powers(IMAGES + 2, 4, 8)
+            denom(IMAGES - 1)
+            pmat(IMAGES - 2, nc.vector)
+            v_transposed(IMAGES - 3)
+            spread_rv(IMAGES - 5)
+            v_rows(IMAGES - 5, pft, "ft")
+            recip(IMAGES - 1)
+            quant_p(IMAGES - 2)
+            pmat(IMAGES - 1, nc.vector)
+            v_transposed(IMAGES - 2)
+            square_vt(IMAGES - 4)
+            copy_rv(IMAGES - 5)
+            final(IMAGES - 5)
+            quant_p(IMAGES - 1)
+            v_transposed(IMAGES - 1)
+            square_vt(IMAGES - 3)
+            powers(IMAGES + 1, 8, 9)
+            spread_rv(IMAGES - 4)
+            v_rows(IMAGES - 4, pft, "ft")
+            square_vt(IMAGES - 2)
+            powers(IMAGES + 2, 8, 9)
+            square_vt(IMAGES - 1)
+            copy_rv(IMAGES - 4)
+            spread_rv(IMAGES - 3)
+            v_rows(IMAGES - 3, pft, "ft")
+            final(IMAGES - 4)
+            powers(IMAGES + 3, 8, 9)
+            copy_rv(IMAGES - 3)
+            powers(IMAGES + 4, 8, 9)
+            final(IMAGES - 3)
+            spread_rv(IMAGES - 2)
+            v_rows(IMAGES - 2, pft, "ft")
+            copy_rv(IMAGES - 2)
+            final(IMAGES - 2)
+            spread_rv(IMAGES - 1)
+            v_rows(IMAGES - 1, pft, "ft")
+            copy_rv(IMAGES - 1)
+            final(IMAGES - 1)

from contextlib import ExitStack

import concourse.mybir as mybir
from concourse.masks import make_identity

FP8X4 = mybir.dt.float8_e4m3fn_x4
BF16 = mybir.dt.bfloat16
F32 = mybir.dt.float32
U32 = mybir.dt.uint32
U8 = mybir.dt.uint8
ACT = mybir.ActivationFunctionType
ALU = mybir.AluOpType
AX = mybir.AxisListType

P = 128
IMAGES = 24
D = 512
N = 512
K = 128
FLOPS = 2 * IMAGES * (K * 512 * N + N * D * N + D * N * K)


def tile_salad_pa_t_kernel(tc, f_clu, h_score, W_s2, b_s2, burst_par, out):
    nc = tc.nc
    with ExitStack() as ctx:
        const = ctx.enter_context(tc.tile_pool(name="const", bufs=1))
        ld = ctx.enter_context(tc.tile_pool(name="ld", bufs=4))
        grp = ctx.enter_context(tc.tile_pool(name="grp", bufs=2))
        qf = ctx.enter_context(tc.tile_pool(name="qf", bufs=7))
        qs = ctx.enter_context(tc.tile_pool(name="qs", bufs=3))
        work = ctx.enter_context(tc.tile_pool(name="work", bufs=3))
        small = ctx.enter_context(tc.tile_pool(name="small", bufs=7))
        junkp = ctx.enter_context(tc.tile_pool(name="junkp", bufs=6))
        pft = ctx.enter_context(tc.psum_pool(name="pft", bufs=2))
        psc = ctx.enter_context(tc.psum_pool(name="psc", bufs=1))
        prn = ctx.enter_context(tc.psum_pool(name="prn", bufs=1))
        psim = ctx.enter_context(tc.psum_pool(name="psim", bufs=2))
        paux = ctx.enter_context(tc.psum_pool(name="paux", bufs=2))

        ident = const.tile([P, P], F32, name="ident")
        make_identity(nc, ident[:])
        w_sb = const.tile([P, 512], BF16, name="w_sb")
        row0 = const.tile([P, 2 * K], BF16, name="row0")
        nc.vector.memset(row0[:], 0.0)
        ones = const.tile([P, P], BF16, name="ones")
        nc.vector.memset(ones[:], 1.0)
        expo = const.tile([P, 9], F32, name="expo")
        nc.vector.memset(expo[:], -0.5)
        bias = const.tile([P, K], F32, name="bias")
        half = const.tile([P, 2], F32, name="half")
        g_w = const.tile([P, 4 * K], BF16, name="g_w", align_bytes=64)
        w_q = const.tile([P, K], U32, name="w_q", align_bytes=64)
        w_s = const.tile([P, K], U8, name="w_s", align_bytes=64)

        def small_loads():
            nc.sync.dma_start(out=w_sb[:], in_=W_s2)
            nc.sync.dma_start(out=row0[0:1, 0:K], in_=b_s2.unsqueeze(0))
            nc.sync.dma_start(out=row0[0:1, K : K + 3], in_=burst_par.unsqueeze(0))

        def constants():
            sps = paux.tile([P, K + 4], F32, tag="aux", name="sps")
            nc.tensor.matmul(
                out=sps[:], lhsT=ones[:], rhs=row0[:, 0 : K + 4], start=True, stop=True
            )
            nc.vector.tensor_copy(out=bias[:], in_=sps[:, 0:K])
            nc.vector.tensor_scalar_mul(out=half[:], in0=sps[:, K : K + 2], scalar1=0.5)
            nc.vector.tensor_copy(out=expo[:, 4:8], in_=sps[:, K + 2 : K + 3].to_broadcast([P, 4]))
            wps = paux.tile([P, 2, P], F32, tag="aux", name="wps")
            w32 = w_sb[:].bitcast(F32).rearrange("k (p u) -> k p u", u=2)
            for u in range(2):
                nc.tensor.transpose(wps[:, u, :], w32[:, :, u], ident[:])
            nc.vector.tensor_copy(
                out=g_w[:].bitcast(F32).rearrange("p (k u) -> p k u", u=2),
                in_=wps[:].rearrange("p u k -> p k u"),
            )
            nc.vector.quantize_mx(out=w_q[:].bitcast(FP8X4), scales=w_s[:], in_=g_w[:])

        def junk():
            return junkp.tile([P, 512], BF16, tag="junk", name="junk_s")

        st = {}

        def load_f(i):
            f_sb = ld.tile([P, 4 * N], BF16, tag="f", name="f_sb", bufs=5)
            nc.sync.dma_start(out=f_sb[:], in_=f_clu[i].rearrange("(p j) n -> p (j n)", j=4))
            st[("f", i)] = f_sb

        def load_h(i):
            h_sb = ld.tile([P, 4 * N], BF16, tag="h", name="h_sb", bufs=4)
            nc.sync.dma_start(out=h_sb[:], in_=h_score[i].rearrange("(p j) n -> p (j n)", j=4))
            st[("h", i)] = h_sb

        def transposes(i):
            f32v = st[("f", i)][:].bitcast(F32).rearrange("p (j u q) -> p j u q", j=4, u=2)
            banks = []
            for b in range(2):
                ftb = pft.tile([P, 2, 256], F32, tag="ft", name="ftb")
                for u in range(2):
                    for jj in range(2):
                        nc.tensor.transpose(
                            ftb[:, u, jj * P : (jj + 1) * P], f32v[:, 2 * b + jj, u, :], ident[:]
                        )
                banks.append(ftb)
            st[("ftb", i)] = banks

        def copy_out(i):
            g_t = grp.tile([P, 4 * D], BF16, tag="gt", name="g_t", align_bytes=64)
            g_t32 = g_t[:].bitcast(F32).rearrange("q (c u) -> q c u", u=2)
            for b in range(2):
                nc.scalar.copy(
                    out=g_t32[:, b * 256 : (b + 1) * 256, :],
                    in_=st[("ftb", i)][b][:].rearrange("q u c -> q c u"),
                )
            st[("gt", i)] = g_t

        def quant_ft(i):
            ft_q = qf.tile([P, D], U32, tag="ftq", name="ft_q", align_bytes=64)
            ft_s = qf.tile([P, D], U8, tag="fts", name="ft_s", align_bytes=64)
            nc.vector.quantize_mx(out=ft_q[:].bitcast(FP8X4), scales=ft_s[:], in_=st[("gt", i)][:])
            st[("ftq", i)] = (ft_q, ft_s)

        def squares(i, t):
            if t == 0:
                st[("ss", i)] = small.tile([P, 4], F32, tag="ss", name="ss")
            g_tv = st[("gt", i)][:].rearrange("q (c t) -> q c t", t=4)
            nc.scalar.activation(
                out=junk()[:], in_=g_tv[:, :, t], func=ACT.Square, accum_out=st[("ss", i)][:, t : t + 1]
            )

        def bases(r):
            if ("bases", r) not in st:
                st[("bases", r)] = small.tile([P, 9], F32, tag="bases", name="bases")
            return st[("bases", r)]

        def guard(i):
            nc.vector.tensor_scalar_max(out=bases(i)[:, 0:4], in0=st[("ss", i)][:], scalar1=1e-24)

        def powers(r, first, last):
            if ("pw", r) not in st:
                st[("pw", r)] = small.tile([P, 9], F32, tag="pw", name="pw")
            nc.gpsimd.tensor_tensor(
                out=st[("pw", r)][:, first:last],
                in0=bases(r)[:, first:last],
                in1=expo[:, first:last],
                op=ALU.pow,
            )

        def spread_rn(i):
            rn = st[("pw", i)]
            rnb = prn.tile([P, N], F32, tag="rnb", name="rnb")
            for u in range(2):
                for e in range(2):
                    block = slice((2 * e + u) * P, (2 * e + u + 1) * P)
                    t = 2 * u + e
                    nc.tensor.transpose(
                        rnb[:, block], rn[:, t : t + 1].to_broadcast([P, P]), ident[:]
                    )
            st[("rnb", i)] = rnb

        def fn_mult(i):
            g_f = grp.tile([P, 4 * N], BF16, tag="gf", name="g_f", align_bytes=64)
            nc.vector.tensor_tensor(
                out=g_f[:].rearrange("p (e w j) -> p w j e", e=2, j=4),
                in0=st[("f", i)][:].rearrange("p (j w e) -> p w j e", j=4, e=2),
                in1=st[("rnb", i)][:]
                .rearrange("p (e w) -> p w e", e=2)
                .unsqueeze(2)
                .to_broadcast([P, 2 * P, 4, 2]),
                op=ALU.mult,
            )
            st[("gf", i)] = g_f

        def quant_fn(i):
            fn_q = qs.tile([P, N], U32, tag="fnq", name="fn_q", align_bytes=64)
            fn_s = qs.tile([P, N], U8, tag="fns", name="fn_s", align_bytes=64)
            nc.vector.quantize_mx(out=fn_q[:].bitcast(FP8X4), scales=fn_s[:], in_=st[("gf", i)][:])
            st[("fnq", i)] = (fn_q, fn_s)
            st[("ta", i)] = small.tile([P, 4], F32, tag="ta", name="ta")

        def h_regroup(i):
            g_h = grp.tile([P, 4 * N], BF16, tag="gh", name="g_h", align_bytes=64)
            nc.vector.tensor_copy(
                out=g_h[:].rearrange("p (e w j) -> p w j e", e=2, j=4),
                in_=st[("h", i)][:].rearrange("p (j w e) -> p w j e", j=4, e=2),
            )
            st[("gh", i)] = g_h

        def quant_h(i):
            h_q = qs.tile([P, N], U32, tag="hq", name="h_q", align_bytes=64)
            h_s = qs.tile([P, N], U8, tag="hs", name="h_s", align_bytes=64)
            nc.vector.quantize_mx(out=h_q[:].bitcast(FP8X4), scales=h_s[:], in_=st[("gh", i)][:])
            st[("hq", i)] = (h_q, h_s)

        def scores(i):
            h_q, h_s = st[("hq", i)]
            sc = psc.tile([P, 4 * K], F32, tag="sc", name="sc")
            for t in range(4):
                cols = slice(t * P, (t + 1) * P)
                nc.tensor.matmul_mx(
                    out=sc[:, t * K : (t + 1) * K],
                    lhsT=h_q[:, cols].bitcast(FP8X4),
                    lhsT_scale=h_s[:, cols],
                    rhs=w_q[:].bitcast(FP8X4),
                    rhs_scale=w_s[:],
                    start=True,
                    stop=True,
                )
            st[("sc", i)] = sc

        def bias_add(i):
            sb = work.tile([P, 4 * K], F32, tag="sb", name="sb")
            nc.vector.tensor_tensor(
                out=sb[:].rearrange("q (t k) -> q t k", t=4),
                in0=st[("sc", i)][:].rearrange("q (t k) -> q t k", t=4),
                in1=bias[:].unsqueeze(1).to_broadcast([P, 4, K]),
                op=ALU.add,
            )
            st[("sb", i)] = sb

        def row_max(i):
            nm = small.tile([P, 4], F32, tag="nm", name="nm")
            nc.vector.tensor_reduce(
                out=nm[:],
                in_=st[("sb", i)][:].rearrange("q (t k) -> q t k", t=4),
                axis=AX.X,
                op=ALU.max,
                negate=True,
            )
            st[("nm", i)] = nm

        def exps(i):
            sb = st[("sb", i)]
            nm = st[("nm", i)]
            e = work.tile([P, 4 * K], F32, tag="e", name="e", bufs=5)
            se = small.tile([P, 4], F32, tag="se", name="se")
            for t in range(4):
                cols = slice(t * K, (t + 1) * K)
                nc.scalar.activation(
                    out=e[:, cols],
                    in_=sb[:, cols],
                    func=ACT.Exp,
                    bias=nm[:, t : t + 1],
                    scale=1.0,
                    accum_out=se[:, t : t + 1],
                )
            st[("e", i)] = (e, se)

        def sim(i, t):
            fn_q, fn_s = st[("fnq", i)]
            cols = slice(t * P, (t + 1) * P)
            sm = psim.tile([P, N], F32, tag="sim", name="sm")
            nc.tensor.matmul_mx(
                out=sm[:],
                lhsT=fn_q[:, cols].bitcast(FP8X4),
                lhsT_scale=fn_s[:, cols],
                rhs=fn_q[:].bitcast(FP8X4),
                rhs_scale=fn_s[:],
                start=True,
                stop=True,
            )
            st[("sm", i, t)] = sm

        def tanh(i, t):
            nc.scalar.activation(
                out=junk()[:],
                in_=st[("sm", i, t)][:],
                func=ACT.Tanh,
                bias=half[:, 1:2],
                scale=half[:, 0:1],
                accum_out=st[("ta", i)][:, t : t + 1],
            )

        def burst(i):
            nc.scalar.activation(
                out=bases(i + 3)[:, 4:8],
                in_=st[("ta", i)][:],
                func=ACT.Copy,
                bias=0.5 * N,
                scale=0.5,
            )

        def denom(i):
            den = small.tile([P, 4], F32, tag="den", name="den")
            nc.vector.scalar_tensor_tensor(
                out=den[:],
                in0=st[("pw", i + 3)][:, 4:8],
                scalar=1e-6,
                in1=st[("e", i)][1][:],
                op0=ALU.add,
                op1=ALU.mult,
            )
            st[("den", i)] = den

        def recip(i):
            c = small.tile([P, 4], F32, tag="c", name="c")
            nc.vector.reciprocal(out=c[:], in_=st[("den", i)][:])
            st[("c", i)] = c

        def pmat(i, engine):
            e = st[("e", i)][0]
            c = st[("c", i)]
            g_p = grp.tile([P, 4 * K], BF16, tag="gp", name="g_p", align_bytes=64)
            engine.tensor_tensor(
                out=g_p[:].rearrange("q (k u e) -> q k u e", u=2, e=2),
                in0=e[:].rearrange("q (e u k) -> q k u e", u=2, e=2),
                in1=c[:].rearrange("q (e u) -> q u e", e=2).unsqueeze(1).to_broadcast([P, K, 2, 2]),
                op=ALU.mult,
            )
            st[("gp", i)] = g_p

        def quant_p(i):
            p_q = qs.tile([P, K], U32, tag="pq", name="p_q", bufs=6, align_bytes=64)
            p_s = qs.tile([P, K], U8, tag="ps", name="p_s", bufs=6, align_bytes=64)
            nc.vector.quantize_mx(out=p_q[:].bitcast(FP8X4), scales=p_s[:], in_=st[("gp", i)][:])
            st[("pq", i)] = (p_q, p_s)

        def v_transposed(i):
            ft_q, ft_s = st[("ftq", i)]
            p_q, p_s = st[("pq", i)]
            vt = paux.tile([P, D], F32, tag="aux", name="vt")
            nc.tensor.matmul_mx(
                out=vt[:],
                lhsT=p_q[:].bitcast(FP8X4),
                lhsT_scale=p_s[:],
                rhs=ft_q[:].bitcast(FP8X4),
                rhs_scale=ft_s[:],
                start=True,
                stop=True,
            )
            st[("vt", i)] = vt

        def square_vt(i):
            nc.scalar.activation(
                out=junk()[:],
                in_=st[("vt", i)][:],
                func=ACT.Square,
                accum_out=bases(i + 5)[:, 8:9],
            )

        def spread_rv(i):
            rvp = paux.tile([P, K], F32, tag="aux", name="rvp")
            nc.tensor.transpose(rvp[:], st[("pw", i + 5)][:, 8:9].to_broadcast([P, P]), ident[:])
            st[("rvp", i)] = rvp

        def v_rows(i, pool=paux, tag="aux"):
            ft_q, ft_s = st[("ftq", i)]
            p_q, p_s = st[("pq", i)]
            v = pool.tile([P, 4 * K], F32, tag=tag, name="v")
            for j in range(4):
                cols = slice(j * P, (j + 1) * P)
                nc.tensor.matmul_mx(
                    out=v[:, j * K : (j + 1) * K],
                    lhsT=ft_q[:, cols].bitcast(FP8X4),
                    lhsT_scale=ft_s[:, cols],
                    rhs=p_q[:].bitcast(FP8X4),
                    rhs_scale=p_s[:],
                    start=True,
                    stop=True,
                )
            st[("v", i)] = v

        def copy_rv(i):
            rvs = work.tile([P, K], F32, tag="rvs", name="rvs")
            nc.scalar.copy(out=rvs[:], in_=st[("rvp", i)][:])
            st[("rvs", i)] = rvs

        def final(i):
            o = work.tile([P, 4 * K], F32, tag="o", name="o")
            nc.vector.scalar_tensor_tensor(
                out=o[:].rearrange("p (j k) -> p j k", j=4),
                in0=st[("rvs", i)][:].unsqueeze(1).to_broadcast([P, 4, K]),
                scalar=1e12,
                in1=st[("v", i)][:].rearrange("p (j k) -> p j k", j=4),
                op0=ALU.min,
                op1=ALU.mult,
            )
            nc.sync.dma_start(out=out[i].rearrange("(p j) k -> p (j k)", j=4), in_=o[:])

        def on(step, i, *args):
            if 0 <= i < IMAGES:
                step(i, *args)

        with tc.manual_schedule():
            load_f(0)
            small_loads()
            load_h(0)
            for r in range(-1, IMAGES + 0):
                on(load_f, r + 2)
                on(load_h, r + 2)
                on(scores, r - 1)
                on(fn_mult, r - 2)
                on(tanh, r - 3, 0)
                on(tanh, r - 3, 1)
                on(sim, r - 3, 2)
                on(sim, r - 3, 3)
                on(tanh, r - 3, 2)
                on(tanh, r - 3, 3)
                on(bias_add, r - 1)
                on(pmat, r - 5, nc.gpsimd)
                on(copy_out, r)
                on(burst, r - 3)
                on(final, r - 7)
                on(row_max, r - 1)
                on(transposes, r + 1)
                on(spread_rn, r - 1)
                on(spread_rv, r - 6)
                on(exps, r - 2)
                on(denom, r - 4)
                on(quant_fn, r - 2)
                on(quant_p, r - 5)
                on(squares, r, 0)
                on(squares, r, 1)
                on(recip, r - 4)
                on(v_rows, r - 6)
                on(copy_rv, r - 6)
                on(v_transposed, r - 5)
                on(h_regroup, r)
                on(sim, r - 2, 0)
                on(sim, r - 2, 1)
                on(squares, r, 2)
                on(squares, r, 3)
                on(quant_ft, r)
                on(square_vt, r - 5)
                on(quant_h, r)
                on(guard, r)
                if r >= 0:
                    powers(r, 0, 9 if r >= 5 else 8 if r >= 3 else 4)
                if r == -1:
                    constants()
            fn_mult(IMAGES - 2)
            scores(IMAGES - 1)
            tanh(IMAGES - 3, 0)
            tanh(IMAGES - 3, 1)
            sim(IMAGES - 3, 2)
            sim(IMAGES - 3, 3)
            tanh(IMAGES - 3, 2)
            tanh(IMAGES - 3, 3)
            burst(IMAGES - 3)
            final(IMAGES - 7)
            exps(IMAGES - 2)
            powers(IMAGES + 0, 4, 8)
            spread_rn(IMAGES - 1)
            bias_add(IMAGES - 1)
            spread_rv(IMAGES - 6)
            v_rows(IMAGES - 6, pft, "ft")
            row_max(IMAGES - 1)
            quant_fn(IMAGES - 2)
            copy_rv(IMAGES - 6)
            fn_mult(IMAGES - 1)
            sim(IMAGES - 2, 0)
            sim(IMAGES - 2, 1)
            tanh(IMAGES - 2, 0)
            tanh(IMAGES - 2, 1)
            sim(IMAGES - 2, 2)
            sim(IMAGES - 2, 3)
            tanh(IMAGES - 2, 2)
            pmat(IMAGES - 5, nc.vector)
            tanh(IMAGES - 2, 3)
            quant_fn(IMAGES - 1)
            denom(IMAGES - 4)
            quant_p(IMAGES - 5)
            burst(IMAGES - 2)
            sim(IMAGES - 1, 0)
            recip(IMAGES - 4)
            sim(IMAGES - 1, 1)
            powers(IMAGES + 1, 4, 8)
            final(IMAGES - 6)
            tanh(IMAGES - 1, 0)
            v_transposed(IMAGES - 5)
            pmat(IMAGES - 4, nc.vector)
            tanh(IMAGES - 1, 1)
            sim(IMAGES - 1, 2)
            sim(IMAGES - 1, 3)
            denom(IMAGES - 3)
            quant_p(IMAGES - 4)
            square_vt(IMAGES - 5)
            recip(IMAGES - 3)
            denom(IMAGES - 2)
            v_transposed(IMAGES - 4)
            pmat(IMAGES - 3, nc.vector)
            tanh(IMAGES - 1, 2)
            tanh(IMAGES - 1, 3)
            burst(IMAGES - 1)
            exps(IMAGES - 1)
            powers(IMAGES + 0, 8, 9)
            recip(IMAGES - 2)
            quant_p(IMAGES - 3)
            powers(IMAGES + 2, 4, 8)
            denom(IMAGES - 1)
            pmat(IMAGES - 2, nc.vector)
            v_transposed(IMAGES - 3)
            spread_rv(IMAGES - 5)
            v_rows(IMAGES - 5, pft, "ft")
            recip(IMAGES - 1)
            quant_p(IMAGES - 2)
            pmat(IMAGES - 1, nc.vector)
            v_transposed(IMAGES - 2)
            square_vt(IMAGES - 4)
            copy_rv(IMAGES - 5)
            final(IMAGES - 5)
            quant_p(IMAGES - 1)
            v_transposed(IMAGES - 1)
            square_vt(IMAGES - 3)
            powers(IMAGES + 1, 8, 9)
            spread_rv(IMAGES - 4)
            v_rows(IMAGES - 4, pft, "ft")
            square_vt(IMAGES - 2)
            powers(IMAGES + 2, 8, 9)
            square_vt(IMAGES - 1)
            copy_rv(IMAGES - 4)
            spread_rv(IMAGES - 3)
            v_rows(IMAGES - 3, pft, "ft")
            final(IMAGES - 4)
            powers(IMAGES + 3, 8, 9)
            copy_rv(IMAGES - 3)
            powers(IMAGES + 4, 8, 9)
            final(IMAGES - 3)
            spread_rv(IMAGES - 2)
            v_rows(IMAGES - 2, pft, "ft")
            copy_rv(IMAGES - 2)
            final(IMAGES - 2)
            spread_rv(IMAGES - 1)
            v_rows(IMAGES - 1, pft, "ft")
            copy_rv(IMAGES - 1)
            final(IMAGES - 1)
